import numpy as np
import ml_dtypes


def mxq(x, axis, fmt="e4m3"):
    dtype, down = {"e4m3": (ml_dtypes.float8_e4m3fn, 7), "e5m2": (ml_dtypes.float8_e5m2, 14)}[fmt]
    v = np.moveaxis(np.asarray(x, np.float32).astype(ml_dtypes.bfloat16).astype(np.float64), axis, -1)
    blocks = v.reshape(v.shape[:-1] + (-1, 32))
    amax = np.abs(blocks).max(-1, keepdims=True)
    byte = np.maximum(np.where(amax > 0, np.frexp(amax)[1] - 1 + 127, 0) - down, 1)
    scale = np.exp2(byte - 127.0)
    codes = (blocks / scale).astype(np.float32).astype(dtype).astype(np.float64)
    return np.moveaxis((codes * scale).reshape(v.shape), -1, axis)


WIDE = False


def mx_kscale(k):
    if not WIDE:
        return np.ones(k)
    levels = np.array([10, -10, 5, -5, 0])
    if k % 512:
        return np.exp2(np.random.permutation(np.resize(levels, k // 32))).repeat(32)
    a = np.empty((k // 512, 16))
    for p in range(k // 512):
        a[p, :8] = np.random.permutation(np.resize(levels, 8))
        for g in range(8):
            far = levels[np.abs(levels - a[p, g]) >= 10]
            a[p, g + 8] = far[np.random.randint(len(far))]
    return np.exp2(a.ravel()).repeat(32)


BF16 = ml_dtypes.bfloat16


def bf(x):
    return np.asarray(x, np.float32).astype(BF16)


def f64(x):
    return np.asarray(x).astype(np.float64)


B, N, F, DIM, H, DH, D3 = 4, 196, 16, 512, 1, 64, 512
W = H * D3
SCALE = 1.0 / (np.sqrt(DH) * H)
QS = np.sqrt(1.5 / (SCALE * np.sqrt(D3)))


def setup_inputs():
    s, t = mx_kscale(DIM), mx_kscale(D3)
    th = np.tile(t, H)
    return {"x": bf(np.random.standard_normal((B, N * F, DIM)) * s),
            "Wq": bf(np.random.standard_normal((DIM, W)) * QS / np.sqrt(DIM) / s[:, None] * th),
            "bq": bf(np.random.standard_normal(W) * 0.2 * QS * th),
            "k": bf(np.random.standard_normal((B, H, N, F, D3)) * QS / t)}


def reference(x, Wq, bq, k):
    y = (mxq(f64(x), 2, "e4m3") @ mxq(f64(Wq), 0, "e4m3")) + f64(bq)
    q = y.reshape(B, F, N, H, D3).transpose(0, 3, 2, 1, 4)
    s = (mxq(q, 4, "e4m3") @ mxq(f64(k), 4, "e4m3").transpose(0, 1, 2, 4, 3)) * SCALE
    e = np.exp(s - s.max(-1, keepdims=True))
    return e / e.sum(-1, keepdims=True)

@@ -1,0 +1,420 @@
+from contextlib import ExitStack
+
+import concourse.mybir as mybir
+from concourse.masks import make_identity
+
+F32 = mybir.dt.float32
+BF16 = mybir.dt.bfloat16
+U32 = mybir.dt.uint32
+U8 = mybir.dt.uint8
+FP8X4 = mybir.dt.float8_e4m3fn_x4
+ALU = mybir.AluOpType
+ACT = mybir.ActivationFunctionType
+AX = mybir.AxisListType
+
+P = 128
+E = 512
+STEPS = 98
+FLOPS = 2 * 12544 * 512 * 512 + 2 * 784 * 16 * 16 * 512
+BIG = 2.0 ** 100
+
+BLOCKS = [(0, 2), (2, 4)] + [(6 + 8 * i, 8) for i in range(11)] + [(94, 4)]
+UNITS = {8: ((0, 4), (4, 2), (6, 7)), 4: ((0, 2), None, (2, 3)), 2: ((0, 1), None, (1,))}
+
+
+def tile_dividedspacetimeattention_pa_t_kernel(tc, x, Wq, bq, k, out):
+    nc = tc.nc
+    nb = len(BLOCKS)
+    xv = x.rearrange("b (q t) e -> (b q) t e", t=STEPS)
+    kv = k.rearrange("b h (j t) g e -> (t g) (b h j) e", j=2, t=STEPS)
+    ov = out.rearrange("b h (j t) f g -> (t f) (b h j) g", j=2, t=STEPS)
+
+    with ExitStack() as ctx:
+        const = ctx.enter_context(tc.tile_pool(name="const", bufs=1))
+        sb = ctx.enter_context(tc.tile_pool(name="sb", bufs=2))
+        ps = ctx.enter_context(tc.psum_pool(name="ps", bufs=1))
+        ctx.enter_context(tc.manual_schedule())
+
+        x_sb = {}
+        k_sb = {}
+        xg = {}
+        kg = {}
+        xc = {}
+        kc = {}
+        qp = {}
+        qg = {}
+        qc = {}
+        s_sb = {}
+        d_sb = {}
+        e_sb = {}
+        r_sb = {}
+        tr_of = {}
+        y_of = {}
+        sc_of = {}
+
+        def load(b):
+            t0, T = BLOCKS[b]
+            L = 8 // T
+            xt = sb.tile([P, 8 * E], BF16, name="x_sb", tag="x_sb", bufs=3)
+            nc.sync.dma_start(
+                out=xt[:, 0 : E * T].rearrange("p (t e) -> p t e", e=E),
+                in_=xv[:, t0 : t0 + T, :],
+            )
+            x_sb[b] = xt
+            kt = sb.tile([P, 8 * E], BF16, name="k_sb", tag="k_sb", bufs=3)
+            k3 = kt[:, 0 : E * T].rearrange("p (h e) -> p h e", e=E)
+            rows = kv[16 * t0 : 16 * (t0 + T), :, :].rearrange("r (h l) e -> l r h e", l=L)
+            for l in range(L):
+                nc.sync.dma_start(out=k3[16 * T * l : 16 * T * (l + 1), :, :], in_=rows[l])
+            k_sb[b] = kt
+
+        load(0)
+        wraw = const.tile([P, 4, E], BF16, name="wraw")
+        nc.sync.dma_start(out=wraw[:], in_=Wq.rearrange("(p j) n -> p j n", j=4))
+        b_bf = const.tile([P, 4], BF16, name="b_bf")
+        nc.scalar.dma_start(out=b_bf[:], in_=bq.rearrange("(p j) -> p j", j=4))
+        load(1)
+
+        ident = const.tile([P, P], F32, name="ident")
+        make_identity(nc, ident[:])
+        zero = const.tile([P, 8], F32, name="zero")
+        nc.vector.memset(zero[:], 0.0)
+        warm = const.tile([P, 8], F32, name="warm")
+        nc.scalar.activation(out=warm[:], in_=zero[:], func=ACT.Exp)
+
+        perm = const.tile([P, P], F32, name="perm")
+        nc.vector.tensor_copy(
+            out=perm[:].rearrange("p (b j f) -> p b j f", b=4, j=2, f=16),
+            in_=ident[:].rearrange("p (b f j) -> p b j f", b=4, f=16, j=2),
+        )
+        ag = const.tile([P, 4 * P], BF16, name="ag", align_bytes=64)
+        bg = const.tile([P, 4 * P], BF16, name="bg", align_bytes=64)
+        nc.vector.memset(ag[:], 0.0)
+        nc.vector.memset(bg[:], 0.0)
+        slot = ident[:, 0:8].unsqueeze(2).to_broadcast([P, 8, 16])
+        nc.vector.tensor_copy(
+            out=ag[:].rearrange("p (s f j) -> p s f j", s=8, f=16, j=4)[:, :, :, 0], in_=slot
+        )
+        nc.vector.tensor_scalar(
+            out=bg[:].rearrange("p (s f j) -> p s f j", s=8, f=16, j=4)[:, :, :, 0],
+            in0=slot,
+            scalar1=-1.0,
+            scalar2=BIG,
+            op0=ALU.add,
+            op1=ALU.mult,
+        )
+        ac = const.tile([P, P], U32, name="ac", align_bytes=64)
+        asc = const.tile([P, P], U8, name="asc", align_bytes=64)
+        bc = const.tile([P, P], U32, name="bc", align_bytes=64)
+        bsc = const.tile([P, P], U8, name="bsc", align_bytes=64)
+        nc.vector.quantize_mx(out=ac[:].bitcast(FP8X4), scales=asc[:], in_=ag[:])
+        nc.vector.quantize_mx(out=bc[:].bitcast(FP8X4), scales=bsc[:], in_=bg[:])
+
+        b32 = const.tile([P, 4], F32, name="b32")
+        nc.vector.tensor_copy(out=b32[:], in_=b_bf[:])
+        wg = const.tile([P, 4 * E], BF16, name="wg", align_bytes=64)
+        wgv = wg[:].rearrange("p (t m j) -> p t m j", t=4, m=P, j=4)
+        wrv = wraw[:].rearrange("p j (m t) -> p t m j", m=P, t=4)
+        for t in range(4):
+            nc.vector.tensor_copy(out=wgv[:, t], in_=wrv[:, t])
+        wc = const.tile([P, E], U32, name="wc", align_bytes=64)
+        ws = const.tile([P, E], U8, name="ws", align_bytes=64)
+        nc.vector.quantize_mx(out=wc[:].bitcast(FP8X4), scales=ws[:], in_=wg[:])
+
+        def size(b):
+            return BLOCKS[b][1]
+
+        def tp(b, w, m):
+            T = size(b)
+            if m >= T // 2:
+                return
+            tr = ps.tile([P, 512], F32, name="tr", tag="tr", bufs=4)
+            if w == "x":
+                src = x_sb[b][:].bitcast(F32)
+                trv = tr[:].rearrange("p (u c s f) -> p u c s f", u=2, c=8, s=2, f=16)
+            else:
+                src = k_sb[b][:].bitcast(F32)
+            for s in range(2):
+                for u in range(2):
+                    c0 = 256 * (2 * m + s)
+                    words = src[:, c0 + u : c0 + 256 : 2]
+                    if w == "x":
+                        nc.tensor.transpose(trv[:, u, :, s, :], words, perm[:])
+                    else:
+                        o = 256 * s + 128 * u
+                        nc.tensor.transpose(tr[:, o : o + 128], words, ident[:])
+            tr_of[(w, b, m)] = tr
+
+        def cp(b, w, m):
+            T = size(b)
+            if m >= T // 2:
+                return
+            if w == "x":
+                if m == 0:
+                    xg[b] = sb.tile([P, 8 * E], BF16, name="xg", tag="xg", bufs=2, align_bytes=64)
+                gv = xg[b][:].bitcast(F32)[:, 0 : 256 * T].rearrange(
+                    "p (c m q u) -> p c m q u", c=8, m=T // 2, q=32, u=2
+                )
+                nc.scalar.copy(
+                    out=gv[:, :, m, :, :],
+                    in_=tr_of[(w, b, m)][:].rearrange("p (u c q) -> p c q u", u=2, c=8, q=32),
+                )
+            else:
+                if m == 0:
+                    kg[b] = sb.tile([P, 8 * E], BF16, name="kg", tag="kg", bufs=2, align_bytes=64)
+                nc.scalar.copy(
+                    out=kg[b][:].bitcast(F32)[:, 512 * m : 512 * m + 512].rearrange(
+                        "p (s q u) -> p s q u", s=2, q=P, u=2
+                    ),
+                    in_=tr_of[(w, b, m)][:].rearrange("p (s u q) -> p s q u", s=2, u=2, q=P),
+                )
+
+        def quant(src, b, store, tag, bufs):
+            T = size(b)
+            c = sb.tile([P, 1024], U32, name=tag + "c", tag=tag + "c", bufs=bufs, align_bytes=64)
+            s = sb.tile([P, 1024], U8, name=tag + "s", tag=tag + "s", bufs=bufs, align_bytes=64)
+            nc.vector.quantize_mx(
+                out=c[:, 0 : P * T].bitcast(FP8X4), scales=s[:, 0 : P * T], in_=src[b][:, 0 : E * T]
+            )
+            store[b] = (c, s)
+
+        def m1_pass(b, y, o, j, g0, n):
+            c, s = xc[b]
+            nc.tensor.matmul_mx(
+                out=y[:, o : o + n],
+                lhsT=wc[:, P * j : P * j + P].bitcast(FP8X4),
+                lhsT_scale=ws[:, P * j : P * j + P],
+                rhs=c[:, P * g0 : P * g0 + n].bitcast(FP8X4),
+                rhs_scale=s[:, P * g0 : P * g0 + n],
+                start=True,
+                stop=True,
+            )
+
+        def m1s(b, unit, js):
+            g0, ng = unit
+            n = P * ng
+            per = 512 // n
+            for j in js:
+                if j % per == 0:
+                    y_of[(b, g0, j // per)] = ps.tile([P, 512], F32, name="y", tag="y", bufs=3)
+                m1_pass(b, y_of[(b, g0, j // per)], n * (j % per), j, g0, n)
+
+        def act(b, unit, js):
+            g0, ng = unit
+            n = P * ng
+            per = 512 // n
+            for j in js:
+                if j == 0:
+                    qp[(b, g0)] = sb.tile([P, 4, n], BF16, name="qp%d" % ng, tag="qp%d" % ng, bufs=2)
+                o = n * (j % per)
+                nc.scalar.activation(
+                    out=qp[(b, g0)][:, j, :],
+                    in_=y_of[(b, g0, j // per)][:, o : o + n],
+                    func=ACT.Identity,
+                    bias=b32[:, j : j + 1],
+                    scale=1.0,
+                )
+
+        def rg(b, unit):
+            g0, ng = unit
+            nc.vector.tensor_copy(
+                out=qg[b][:, E * g0 : E * (g0 + ng)].rearrange("p (c i j) -> p c j i", i=4, j=4),
+                in_=qp[(b, g0)][:].rearrange("p j (c i) -> p c j i", i=4),
+            )
+
+        def m1v(b, g):
+            y = ps.tile([P, 512], F32, name="y", tag="y", bufs=3)
+            for j in range(4):
+                m1_pass(b, y, P * j, j, g, P)
+            y_of[(b, g)] = y
+
+        def vd(b, g):
+            nc.vector.tensor_tensor(
+                out=qg[b][:, E * g : E * g + E].rearrange("p (q j) -> p q j", j=4),
+                in0=y_of[(b, g)][:].rearrange("p (j q) -> p q j", j=4),
+                in1=b32[:].unsqueeze(1).to_broadcast([P, P, 4]),
+                op=ALU.add,
+            )
+
+        def qq(b, h):
+            w = size(b) // 2
+            if h == 0:
+                c = sb.tile([P, 1024], U32, name="qc", tag="qc", bufs=2, align_bytes=64)
+                s = sb.tile([P, 1024], U8, name="qs", tag="qs", bufs=2, align_bytes=64)
+                qc[b] = (c, s)
+            c, s = qc[b]
+            nc.vector.quantize_mx(
+                out=c[:, P * w * h : P * w * (h + 1)].bitcast(FP8X4),
+                scales=s[:, P * w * h : P * w * (h + 1)],
+                in_=qg[b][:, E * w * h : E * w * (h + 1)],
+            )
+
+        def m2(b, h, part):
+            w = size(b) // 2
+            cut = (w + 1) // 2
+            lanes = range(0, cut) if part == 0 else range(cut, w)
+            c, s = qc[b]
+            c2, s2 = kc[b]
+            if part == 0:
+                sc_of[(b, h)] = ps.tile([P, 512], F32, name="sc", tag="sc", bufs=1)
+            sc = sc_of[(b, h)]
+            for i in lanes:
+                g = h * w + i
+                nc.tensor.matmul_mx(
+                    out=sc[:, P * i : P * i + P],
+                    lhsT=c[:, P * g : P * g + P].bitcast(FP8X4),
+                    lhsT_scale=s[:, P * g : P * g + P],
+                    rhs=c2[:, P * g : P * g + P].bitcast(FP8X4),
+                    rhs_scale=s2[:, P * g : P * g + P],
+                    start=True,
+                    stop=False,
+                )
+                nc.tensor.matmul_mx(
+                    out=sc[:, P * i : P * i + P],
+                    lhsT=ac[:].bitcast(FP8X4),
+                    lhsT_scale=asc[:],
+                    rhs=bc[:].bitcast(FP8X4),
+                    rhs_scale=bsc[:],
+                    start=False,
+                    stop=True,
+                )
+
+        def red(b, h):
+            w = size(b) // 2
+            if h == 0:
+                s_sb[b] = sb.tile([P, 128], F32, name="s_sb", tag="s_sb", bufs=3)
+            nc.vector.tensor_reduce(
+                out=s_sb[b][:, 16 * w * h : 16 * w * (h + 1)].rearrange("p (l g) -> p l g", g=16),
+                in_=sc_of[(b, h)][:, 0 : P * w].rearrange("p (l t g) -> p l g t", t=8, g=16),
+                axis=AX.X,
+                op=ALU.max,
+            )
+
+        def shift(b):
+            T = size(b)
+            s3 = s_sb[b][:, 0 : 16 * T].rearrange("p (l g) -> p l g", g=16)
+            mx = sb.tile([P, 8], F32, name="mx", tag="mx", bufs=2)
+            nc.vector.tensor_reduce(out=mx[:, 0:T], in_=s3, axis=AX.X, op=ALU.max)
+            d = sb.tile([P, 128], F32, name="d_sb", tag="d_sb", bufs=2)
+            nc.gpsimd.tensor_tensor(
+                out=d[:, 0 : 16 * T].rearrange("p (l g) -> p l g", g=16),
+                in0=s3,
+                in1=mx[:, 0:T].unsqueeze(2).to_broadcast([P, T, 16]),
+                op=ALU.subtract,
+            )
+            d_sb[b] = d
+
+        def expo(b):
+            T = size(b)
+            ex = sb.tile([P, 128], F32, name="e_sb", tag="e_sb", bufs=2)
+            nc.scalar.activation(
+                out=ex[:, 0 : 16 * T], in_=d_sb[b][:, 0 : 16 * T], func=ACT.Exp, scale=0.125
+            )
+            e_sb[b] = ex
+
+        def finish(b):
+            t0, T = BLOCKS[b]
+            L = 8 // T
+            e3 = e_sb[b][:, 0 : 16 * T].rearrange("p (l g) -> p l g", g=16)
+            z = sb.tile([P, 8], F32, name="z", tag="z", bufs=2)
+            nc.vector.tensor_reduce(out=z[:, 0:T], in_=e3, axis=AX.X, op=ALU.add)
+            r = sb.tile([P, 8], F32, name="r", tag="r", bufs=2)
+            nc.vector.reciprocal(out=r[:, 0:T], in_=z[:, 0:T])
+            o = sb.tile([P, 128], F32, name="o_sb", tag="o_sb", bufs=3)
+            o3 = o[:, 0 : 16 * T].rearrange("p (l g) -> p l g", g=16)
+            nc.gpsimd.tensor_tensor(
+                out=o3, in0=e3, in1=r[:, 0:T].unsqueeze(2).to_broadcast([P, T, 16]), op=ALU.mult
+            )
+            rows = ov[16 * t0 : 16 * (t0 + T), :, :].rearrange("r (h l) g -> l r h g", l=L)
+            for l in range(L):
+                nc.sync.dma_start(out=rows[l], in_=o3[16 * T * l : 16 * T * (l + 1), :, :])
+
+        def ok(b):
+            return 0 <= b < nb
+
+        for w in ("x", "k"):
+            for m in range(4):
+                tp(0, w, m)
+            for m in range(4):
+                cp(0, w, m)
+        quant(xg, 0, xc, "x", 2)
+
+        for n in range(nb + 3):
+            a, b1, b2, nx = n, n - 1, n - 2, n + 1
+            ua = UNITS[size(a)] if ok(a) else None
+            u1 = UNITS[size(b1)] if ok(b1) else None
+            if ok(n + 2):
+                load(n + 2)
+            if ok(nx):
+                tp(nx, "x", 0)
+                tp(nx, "x", 1)
+            if ok(a):
+                qg[a] = sb.tile([P, 8 * E], BF16, name="qg", tag="qg", bufs=3, align_bytes=64)
+                m1s(a, ua[0], (0, 1))
+            if ok(b1):
+                m2(b1, 0, 0)
+            if ok(nx):
+                cp(nx, "x", 0)
+                cp(nx, "x", 1)
+            if ok(a):
+                act(a, ua[0], (0, 1))
+            if ok(b1):
+                for g in u1[2]:
+                    vd(b1, g)
+            if ok(b2):
+                red(b2, 1)
+            if ok(b1) and u1[1]:
+                rg(b1, u1[1])
+            if ok(a):
+                quant(kg, a, kc, "k", 3)
+            if ok(b1):
+                qq(b1, 1)
+            if ok(b2):
+                shift(b2)
+            if ok(nx):
+                tp(nx, "x", 2)
+                tp(nx, "x", 3)
+            if ok(a):
+                m1s(a, ua[0], (2, 3))
+            if ok(b1):
+                m2(b1, 0, 1)
+            if ok(nx):
+                cp(nx, "x", 2)
+                cp(nx, "x", 3)
+            if ok(a):
+                act(a, ua[0], (2, 3))
+            if ok(b2):
+                expo(b2)
+            if ok(b1):
+                red(b1, 0)
+            if ok(nx):
+                tp(nx, "k", 0)
+                tp(nx, "k", 1)
+            if ok(a) and ua[1]:
+                m1s(a, ua[1], (0, 1, 2, 3))
+            if ok(b1):
+                m2(b1, 1, 0)
+            if ok(nx):
+                cp(nx, "k", 0)
+                cp(nx, "k", 1)
+            if ok(a) and ua[1]:
+                act(a, ua[1], (0, 1, 2, 3))
+            if ok(a):
+                rg(a, ua[0])
+            if ok(nx):
+                quant(xg, nx, xc, "x", 2)
+            if ok(a):
+                qq(a, 0)
+            if ok(b2):
+                finish(b2)
+            if ok(nx):
+                tp(nx, "k", 2)
+                tp(nx, "k", 3)
+            if ok(a):
+                for g in ua[2]:
+                    m1v(a, g)
+            if ok(b1):
+                m2(b1, 1, 1)
+            if ok(nx):
+                cp(nx, "k", 2)
+                cp(nx, "k", 3)

@@ -18,8 +18,9 @@ STEPS = 98
 FLOPS = 2 * 12544 * 512 * 512 + 2 * 784 * 16 * 16 * 512
 BIG = 2.0 ** 100
 
-BLOCKS = [(0, 2), (2, 4)] + [(6 + 8 * i, 8) for i in range(11)] + [(94, 4)]
-UNITS = {8: ((0, 4), (4, 2), (6, 7)), 4: ((0, 2), None, (2, 3)), 2: ((0, 1), None, (1,))}
+
+BLOCKS = [(0, 2)] + [(2 + 4 * i, 4) for i in range(24)]
+SPLIT = {2: ((0, 1), (1,)), 40: ((0, 3), (3,)), 41: ((0, 3), (3,))}
 
 
 def tile_dividedspacetimeattention_pa_t_kernel(tc, x, Wq, bq, k, out):
@@ -47,6 +48,7 @@ def tile_dividedspacetimeattention_pa_t_kernel(tc, x, Wq, bq, k, out):
         s_sb = {}
         d_sb = {}
         e_sb = {}
+        mx_sb = {}
         r_sb = {}
         tr_of = {}
         y_of = {}
@@ -55,13 +57,13 @@ def tile_dividedspacetimeattention_pa_t_kernel(tc, x, Wq, bq, k, out):
         def load(b):
             t0, T = BLOCKS[b]
             L = 8 // T
-            xt = sb.tile([P, 8 * E], BF16, name="x_sb", tag="x_sb", bufs=3)
+            xt = sb.tile([P, 4 * E], BF16, name="x_sb", tag="x_sb", bufs=6)
             nc.sync.dma_start(
                 out=xt[:, 0 : E * T].rearrange("p (t e) -> p t e", e=E),
                 in_=xv[:, t0 : t0 + T, :],
             )
             x_sb[b] = xt
-            kt = sb.tile([P, 8 * E], BF16, name="k_sb", tag="k_sb", bufs=3)
+            kt = sb.tile([P, 4 * E], BF16, name="k_sb", tag="k_sb", bufs=6)
             k3 = kt[:, 0 : E * T].rearrange("p (h e) -> p h e", e=E)
             rows = kv[16 * t0 : 16 * (t0 + T), :, :].rearrange("r (h l) e -> l r h e", l=L)
             for l in range(L):
@@ -74,6 +76,7 @@ def tile_dividedspacetimeattention_pa_t_kernel(tc, x, Wq, bq, k, out):
         b_bf = const.tile([P, 4], BF16, name="b_bf")
         nc.scalar.dma_start(out=b_bf[:], in_=bq.rearrange("(p j) -> p j", j=4))
         load(1)
+        load(2)
 
         ident = const.tile([P, P], F32, name="ident")
         make_identity(nc, ident[:])
@@ -124,16 +127,15 @@ def tile_dividedspacetimeattention_pa_t_kernel(tc, x, Wq, bq, k, out):
         def size(b):
             return BLOCKS[b][1]
 
+        def split(b):
+            return SPLIT[2] if size(b) == 2 else SPLIT[40 + b % 2]
+
         def tp(b, w, m):
-            T = size(b)
-            if m >= T // 2:
+            if m >= size(b) // 2:
                 return
             tr = ps.tile([P, 512], F32, name="tr", tag="tr", bufs=4)
-            if w == "x":
-                src = x_sb[b][:].bitcast(F32)
-                trv = tr[:].rearrange("p (u c s f) -> p u c s f", u=2, c=8, s=2, f=16)
-            else:
-                src = k_sb[b][:].bitcast(F32)
+            src = (x_sb if w == "x" else k_sb)[b][:].bitcast(F32)
+            trv = tr[:].rearrange("p (u c s f) -> p u c s f", u=2, c=8, s=2, f=16)
             for s in range(2):
                 for u in range(2):
                     c0 = 256 * (2 * m + s)
@@ -151,7 +153,7 @@ def tile_dividedspacetimeattention_pa_t_kernel(tc, x, Wq, bq, k, out):
                 return
             if w == "x":
                 if m == 0:
-                    xg[b] = sb.tile([P, 8 * E], BF16, name="xg", tag="xg", bufs=2, align_bytes=64)
+                    xg[b] = sb.tile([P, 4 * E], BF16, name="xg", tag="xg", bufs=3, align_bytes=64)
                 gv = xg[b][:].bitcast(F32)[:, 0 : 256 * T].rearrange(
                     "p (c m q u) -> p c m q u", c=8, m=T // 2, q=32, u=2
                 )
@@ -161,7 +163,7 @@ def tile_dividedspacetimeattention_pa_t_kernel(tc, x, Wq, bq, k, out):
                 )
             else:
                 if m == 0:
-                    kg[b] = sb.tile([P, 8 * E], BF16, name="kg", tag="kg", bufs=2, align_bytes=64)
+                    kg[b] = sb.tile([P, 4 * E], BF16, name="kg", tag="kg", bufs=3, align_bytes=64)
                 nc.scalar.copy(
                     out=kg[b][:].bitcast(F32)[:, 512 * m : 512 * m + 512].rearrange(
                         "p (s q u) -> p s q u", s=2, q=P, u=2
@@ -171,8 +173,8 @@ def tile_dividedspacetimeattention_pa_t_kernel(tc, x, Wq, bq, k, out):
 
         def quant(src, b, store, tag, bufs):
             T = size(b)
-            c = sb.tile([P, 1024], U32, name=tag + "c", tag=tag + "c", bufs=bufs, align_bytes=64)
-            s = sb.tile([P, 1024], U8, name=tag + "s", tag=tag + "s", bufs=bufs, align_bytes=64)
+            c = sb.tile([P, 512], U32, name=tag + "c", tag=tag + "c", bufs=bufs, align_bytes=64)
+            s = sb.tile([P, 512], U8, name=tag + "s", tag=tag + "s", bufs=bufs, align_bytes=64)
             nc.vector.quantize_mx(
                 out=c[:, 0 : P * T].bitcast(FP8X4), scales=s[:, 0 : P * T], in_=src[b][:, 0 : E * T]
             )
@@ -190,78 +192,82 @@ def tile_dividedspacetimeattention_pa_t_kernel(tc, x, Wq, bq, k, out):
                 stop=True,
             )
 
-        def m1s(b, unit, js):
-            g0, ng = unit
+        def m1s(b, i):
+            g0, ng = split(b)[0]
             n = P * ng
-            per = 512 // n
-            for j in js:
-                if j % per == 0:
-                    y_of[(b, g0, j // per)] = ps.tile([P, 512], F32, name="y", tag="y", bufs=3)
-                m1_pass(b, y_of[(b, g0, j // per)], n * (j % per), j, g0, n)
+            per = {1: 4, 2: 2, 3: 1, 4: 1}[ng]
+            if per * i >= 4:
+                return
+            y = ps.tile([P, 512], F32, name="y", tag="y", bufs=3)
+            for j in range(per * i, per * i + per):
+                for lo, ln in {1: ((0, 1),), 2: ((0, 2),), 3: ((0, 2), (2, 1)), 4: ((0, 4),)}[ng]:
+                    m1_pass(b, y, n * (j % per) + P * lo, j, g0 + lo, P * ln)
+            y_of[(b, i)] = y
 
-        def act(b, unit, js):
-            g0, ng = unit
+        def act(b, i):
+            g0, ng = split(b)[0]
             n = P * ng
-            per = 512 // n
-            for j in js:
-                if j == 0:
-                    qp[(b, g0)] = sb.tile([P, 4, n], BF16, name="qp%d" % ng, tag="qp%d" % ng, bufs=2)
+            per = {1: 4, 2: 2, 3: 1, 4: 1}[ng]
+            if per * i >= 4:
+                return
+            if i == 0:
+                qp[b] = sb.tile([P, 4, n], BF16, name="qp%d" % ng, tag="qp%d" % ng, bufs=2)
+            for j in range(per * i, per * i + per):
                 o = n * (j % per)
                 nc.scalar.activation(
-                    out=qp[(b, g0)][:, j, :],
-                    in_=y_of[(b, g0, j // per)][:, o : o + n],
+                    out=qp[b][:, j, :],
+                    in_=y_of[(b, i)][:, o : o + n],
                     func=ACT.Identity,
                     bias=b32[:, j : j + 1],
                     scale=1.0,
                 )
 
-        def rg(b, unit):
-            g0, ng = unit
+        def new_q(b):
+            qg[b] = sb.tile([P, 4 * E], BF16, name="qg", tag="qg", bufs=3, align_bytes=64)
+
+        def rg(b):
+            g0, ng = split(b)[0]
             nc.vector.tensor_copy(
                 out=qg[b][:, E * g0 : E * (g0 + ng)].rearrange("p (c i j) -> p c j i", i=4, j=4),
-                in_=qp[(b, g0)][:].rearrange("p j (c i) -> p c j i", i=4),
+                in_=qp[b][:].rearrange("p j (c i) -> p c j i", i=4),
             )
 
-        def m1v(b, g):
+        def m1v(b, i):
+            if i >= len(split(b)[1]):
+                return
             y = ps.tile([P, 512], F32, name="y", tag="y", bufs=3)
             for j in range(4):
-                m1_pass(b, y, P * j, j, g, P)
-            y_of[(b, g)] = y
+                m1_pass(b, y, P * j, j, split(b)[1][i], P)
+            y_of[(b, 4 + i)] = y
 
-        def vd(b, g):
+        def vd(b, i):
+            if i >= len(split(b)[1]):
+                return
+            g = split(b)[1][i]
             nc.vector.tensor_tensor(
                 out=qg[b][:, E * g : E * g + E].rearrange("p (q j) -> p q j", j=4),
-                in0=y_of[(b, g)][:].rearrange("p (j q) -> p q j", j=4),
+                in0=y_of[(b, 4 + i)][:].rearrange("p (j q) -> p q j", j=4),
                 in1=b32[:].unsqueeze(1).to_broadcast([P, P, 4]),
                 op=ALU.add,
             )
 
-        def qq(b, h):
-            w = size(b) // 2
-            if h == 0:
-                c = sb.tile([P, 1024], U32, name="qc", tag="qc", bufs=2, align_bytes=64)
-                s = sb.tile([P, 1024], U8, name="qs", tag="qs", bufs=2, align_bytes=64)
-                qc[b] = (c, s)
-            c, s = qc[b]
+        def qq(b):
+            T = size(b)
+            c = sb.tile([P, 512], U32, name="qc", tag="qc", bufs=3, align_bytes=64)
+            s = sb.tile([P, 512], U8, name="qs", tag="qs", bufs=3, align_bytes=64)
             nc.vector.quantize_mx(
-                out=c[:, P * w * h : P * w * (h + 1)].bitcast(FP8X4),
-                scales=s[:, P * w * h : P * w * (h + 1)],
-                in_=qg[b][:, E * w * h : E * w * (h + 1)],
+                out=c[:, 0 : P * T].bitcast(FP8X4), scales=s[:, 0 : P * T], in_=qg[b][:, 0 : E * T]
             )
+            qc[b] = (c, s)
 
-        def m2(b, h, part):
-            w = size(b) // 2
-            cut = (w + 1) // 2
-            lanes = range(0, cut) if part == 0 else range(cut, w)
+        def m2(b):
             c, s = qc[b]
             c2, s2 = kc[b]
-            if part == 0:
-                sc_of[(b, h)] = ps.tile([P, 512], F32, name="sc", tag="sc", bufs=1)
-            sc = sc_of[(b, h)]
-            for i in lanes:
-                g = h * w + i
+            sc = ps.tile([P, 512], F32, name="sc", tag="sc", bufs=1)
+            sc_of[b] = sc
+            for g in range(size(b)):
                 nc.tensor.matmul_mx(
-                    out=sc[:, P * i : P * i + P],
+                    out=sc[:, P * g : P * g + P],
                     lhsT=c[:, P * g : P * g + P].bitcast(FP8X4),
                     lhsT_scale=s[:, P * g : P * g + P],
                     rhs=c2[:, P * g : P * g + P].bitcast(FP8X4),
@@ -270,7 +276,7 @@ def tile_dividedspacetimeattention_pa_t_kernel(tc, x, Wq, bq, k, out):
                     stop=False,
                 )
                 nc.tensor.matmul_mx(
-                    out=sc[:, P * i : P * i + P],
+                    out=sc[:, P * g : P * g + P],
                     lhsT=ac[:].bitcast(FP8X4),
                     lhsT_scale=asc[:],
                     rhs=bc[:].bitcast(FP8X4),
@@ -279,142 +285,131 @@ def tile_dividedspacetimeattention_pa_t_kernel(tc, x, Wq, bq, k, out):
                     stop=True,
                 )
 
-        def red(b, h):
-            w = size(b) // 2
-            if h == 0:
-                s_sb[b] = sb.tile([P, 128], F32, name="s_sb", tag="s_sb", bufs=3)
+        def pair(b):
+            return (b + 1) // 2, 0 if b % 2 else 16 * size(b - 1) if b else 0
+
+        def width(p):
+            return 16 * sum(size(b) for b in range(nb) if pair(b)[0] == p)
+
+        def red(b):
+            p, c0 = pair(b)
+            if p not in s_sb:
+                s_sb[p] = sb.tile([P, 128], F32, name="s_sb", tag="s_sb", bufs=3)
+            w = size(b)
             nc.vector.tensor_reduce(
-                out=s_sb[b][:, 16 * w * h : 16 * w * (h + 1)].rearrange("p (l g) -> p l g", g=16),
-                in_=sc_of[(b, h)][:, 0 : P * w].rearrange("p (l t g) -> p l g t", t=8, g=16),
+                out=s_sb[p][:, c0 : c0 + 16 * w].rearrange("p (l g) -> p l g", g=16),
+                in_=sc_of[b][:, 0 : P * w].rearrange("p (l t g) -> p l g t", t=8, g=16),
                 axis=AX.X,
                 op=ALU.max,
             )
 
-        def shift(b):
-            T = size(b)
-            s3 = s_sb[b][:, 0 : 16 * T].rearrange("p (l g) -> p l g", g=16)
+        def vec(t, n):
+            return t[:, 0:n].rearrange("p (l g) -> p l g", g=16)
+
+        def smax(p):
+            n = width(p)
             mx = sb.tile([P, 8], F32, name="mx", tag="mx", bufs=2)
-            nc.vector.tensor_reduce(out=mx[:, 0:T], in_=s3, axis=AX.X, op=ALU.max)
+            nc.vector.tensor_reduce(out=mx[:, 0 : n // 16], in_=vec(s_sb[p], n), axis=AX.X, op=ALU.max)
+            mx_sb[p] = mx
+
+        def sub(p):
+            n = width(p)
             d = sb.tile([P, 128], F32, name="d_sb", tag="d_sb", bufs=2)
             nc.gpsimd.tensor_tensor(
-                out=d[:, 0 : 16 * T].rearrange("p (l g) -> p l g", g=16),
-                in0=s3,
-                in1=mx[:, 0:T].unsqueeze(2).to_broadcast([P, T, 16]),
+                out=vec(d, n),
+                in0=vec(s_sb[p], n),
+                in1=mx_sb[p][:, 0 : n // 16].unsqueeze(2).to_broadcast([P, n // 16, 16]),
                 op=ALU.subtract,
             )
-            d_sb[b] = d
+            d_sb[p] = d
 
-        def expo(b):
-            T = size(b)
+        def expo(p):
+            n = width(p)
             ex = sb.tile([P, 128], F32, name="e_sb", tag="e_sb", bufs=2)
-            nc.scalar.activation(
-                out=ex[:, 0 : 16 * T], in_=d_sb[b][:, 0 : 16 * T], func=ACT.Exp, scale=0.125
-            )
-            e_sb[b] = ex
+            nc.scalar.activation(out=ex[:, 0:n], in_=d_sb[p][:, 0:n], func=ACT.Exp, scale=0.125)
+            e_sb[p] = ex
 
-        def finish(b):
-            t0, T = BLOCKS[b]
-            L = 8 // T
-            e3 = e_sb[b][:, 0 : 16 * T].rearrange("p (l g) -> p l g", g=16)
+        def ssum(p):
+            n = width(p)
             z = sb.tile([P, 8], F32, name="z", tag="z", bufs=2)
-            nc.vector.tensor_reduce(out=z[:, 0:T], in_=e3, axis=AX.X, op=ALU.add)
-            r = sb.tile([P, 8], F32, name="r", tag="r", bufs=2)
-            nc.vector.reciprocal(out=r[:, 0:T], in_=z[:, 0:T])
-            o = sb.tile([P, 128], F32, name="o_sb", tag="o_sb", bufs=3)
-            o3 = o[:, 0 : 16 * T].rearrange("p (l g) -> p l g", g=16)
-            nc.gpsimd.tensor_tensor(
-                out=o3, in0=e3, in1=r[:, 0:T].unsqueeze(2).to_broadcast([P, T, 16]), op=ALU.mult
-            )
-            rows = ov[16 * t0 : 16 * (t0 + T), :, :].rearrange("r (h l) g -> l r h g", l=L)
-            for l in range(L):
-                nc.sync.dma_start(out=rows[l], in_=o3[16 * T * l : 16 * T * (l + 1), :, :])
+            nc.vector.tensor_reduce(out=z[:, 0 : n // 16], in_=vec(e_sb[p], n), axis=AX.X, op=ALU.add)
+            r_sb[p] = z
 
-        def ok(b):
-            return 0 <= b < nb
+        def recip(p):
+            n = width(p)
+            r = sb.tile([P, 8], F32, name="r", tag="r", bufs=2)
+            nc.vector.reciprocal(out=r[:, 0 : n // 16], in_=r_sb[p][:, 0 : n // 16])
+            r_sb[p] = r
+
+        def finish(p):
+            n = width(p)
+            o = sb.tile([P, 128], F32, name="o_sb", tag="o_sb", bufs=3)
+            nc.gpsimd.tensor_tensor(
+                out=vec(o, n),
+                in0=vec(e_sb[p], n),
+                in1=r_sb[p][:, 0 : n // 16].unsqueeze(2).to_broadcast([P, n // 16, 16]),
+                op=ALU.mult,
+            )
+            for b in range(nb):
+                if pair(b)[0] == p:
+                    t0, T = BLOCKS[b]
+                    L = 8 // T
+                    c0 = pair(b)[1]
+                    o3 = vec(o, n)[:, c0 // 16 : c0 // 16 + T, :]
+                    rows = ov[16 * t0 : 16 * (t0 + T), :, :].rearrange("r (h l) g -> l r h g", l=L)
+                    for l in range(L):
+                        nc.sync.dma_start(out=rows[l], in_=o3[16 * T * l : 16 * T * (l + 1), :, :])
+
+        def on(f, b, *args):
+            if 0 <= b < nb:
+                f(b, *args)
+
+        def onp(f, b):
+            if 0 <= b < nb and (b + 1 == nb or pair(b + 1)[0] != pair(b)[0]):
+                f(pair(b)[0])
 
         for w in ("x", "k"):
-            for m in range(4):
+            for m in range(2):
                 tp(0, w, m)
-            for m in range(4):
+            for m in range(2):
                 cp(0, w, m)
         quant(xg, 0, xc, "x", 2)
 
-        for n in range(nb + 3):
-            a, b1, b2, nx = n, n - 1, n - 2, n + 1
-            ua = UNITS[size(a)] if ok(a) else None
-            u1 = UNITS[size(b1)] if ok(b1) else None
-            if ok(n + 2):
-                load(n + 2)
-            if ok(nx):
-                tp(nx, "x", 0)
-                tp(nx, "x", 1)
-            if ok(a):
-                qg[a] = sb.tile([P, 8 * E], BF16, name="qg", tag="qg", bufs=3, align_bytes=64)
-                m1s(a, ua[0], (0, 1))
-            if ok(b1):
-                m2(b1, 0, 0)
-            if ok(nx):
-                cp(nx, "x", 0)
-                cp(nx, "x", 1)
-            if ok(a):
-                act(a, ua[0], (0, 1))
-            if ok(b1):
-                for g in u1[2]:
-                    vd(b1, g)
-            if ok(b2):
-                red(b2, 1)
-            if ok(b1) and u1[1]:
-                rg(b1, u1[1])
-            if ok(a):
-                quant(kg, a, kc, "k", 3)
-            if ok(b1):
-                qq(b1, 1)
-            if ok(b2):
-                shift(b2)
-            if ok(nx):
-                tp(nx, "x", 2)
-                tp(nx, "x", 3)
-            if ok(a):
-                m1s(a, ua[0], (2, 3))
-            if ok(b1):
-                m2(b1, 0, 1)
-            if ok(nx):
-                cp(nx, "x", 2)
-                cp(nx, "x", 3)
-            if ok(a):
-                act(a, ua[0], (2, 3))
-            if ok(b2):
-                expo(b2)
-            if ok(b1):
-                red(b1, 0)
-            if ok(nx):
-                tp(nx, "k", 0)
-                tp(nx, "k", 1)
-            if ok(a) and ua[1]:
-                m1s(a, ua[1], (0, 1, 2, 3))
-            if ok(b1):
-                m2(b1, 1, 0)
-            if ok(nx):
-                cp(nx, "k", 0)
-                cp(nx, "k", 1)
-            if ok(a) and ua[1]:
-                act(a, ua[1], (0, 1, 2, 3))
-            if ok(a):
-                rg(a, ua[0])
-            if ok(nx):
-                quant(xg, nx, xc, "x", 2)
-            if ok(a):
-                qq(a, 0)
-            if ok(b2):
-                finish(b2)
-            if ok(nx):
-                tp(nx, "k", 2)
-                tp(nx, "k", 3)
-            if ok(a):
-                for g in ua[2]:
-                    m1v(a, g)
-            if ok(b1):
-                m2(b1, 1, 1)
-            if ok(nx):
-                cp(nx, "k", 2)
-                cp(nx, "k", 3)
+        for n in range(nb + 5):
+            on(load, n + 3)
+            on(tp, n + 1, "x", 0)
+            on(tp, n + 1, "x", 1)
+            on(tp, n + 1, "k", 0)
+            on(tp, n + 1, "k", 1)
+            on(cp, n + 1, "x", 0)
+            on(cp, n + 1, "x", 1)
+            on(cp, n + 1, "k", 0)
+            on(cp, n + 1, "k", 1)
+            if n < nb:
+                new_q(n)
+            on(m1v, n, 0)
+            if n < nb:
+                quant(kg, n, kc, "k", 4)
+            on(red, n - 3)
+            on(rg, n - 1)
+            onp(smax, n - 3)
+            onp(ssum, n - 5)
+            on(vd, n, 0)
+            if n + 1 < nb:
+                quant(xg, n + 1, xc, "x", 2)
+            if 0 < n <= nb:
+                qq(n - 1)
+            onp(sub, n - 3)
+            onp(recip, n - 5)
+            onp(finish, n - 5)
+
+            on(m1s, n, 0)
+            on(m1s, n, 1)
+            on(act, n, 0)
+            on(m2, n - 2)
+            on(m1s, n, 2)
+            on(act, n, 1)
+            on(m1s, n, 3)
+            on(act, n, 2)
+            on(act, n, 3)
+            onp(expo, n - 4)

@@ -19,13 +19,14 @@ FLOPS = 2 * 12544 * 512 * 512 + 2 * 784 * 16 * 16 * 512
 BIG = 2.0 ** 100
 
 
-BLOCKS = [(0, 2)] + [(2 + 4 * i, 4) for i in range(24)]
-SPLIT = {2: ((0, 1), (1,)), 40: ((0, 3), (3,)), 41: ((0, 3), (3,))}
+BLOCKS = [(0, 2), (2, 4)] + [(6 + 8 * i, 8) for i in range(11)] + [(94, 4)]
 
 
 def tile_dividedspacetimeattention_pa_t_kernel(tc, x, Wq, bq, k, out):
     nc = tc.nc
     nb = len(BLOCKS)
+    HALVES = [(b, g, min(4, T)) for b, (t0, T) in enumerate(BLOCKS) for g in range(0, T, 4)]
+    nh = len(HALVES)
     xv = x.rearrange("b (q t) e -> (b q) t e", t=STEPS)
     kv = k.rearrange("b h (j t) g e -> (t g) (b h j) e", j=2, t=STEPS)
     ov = out.rearrange("b h (j t) f g -> (t f) (b h j) g", j=2, t=STEPS)
@@ -57,13 +58,13 @@ def tile_dividedspacetimeattention_pa_t_kernel(tc, x, Wq, bq, k, out):
         def load(b):
             t0, T = BLOCKS[b]
             L = 8 // T
-            xt = sb.tile([P, 4 * E], BF16, name="x_sb", tag="x_sb", bufs=6)
+            xt = sb.tile([P, 8 * E], BF16, name="x_sb", tag="x_sb", bufs=3)
             nc.sync.dma_start(
                 out=xt[:, 0 : E * T].rearrange("p (t e) -> p t e", e=E),
                 in_=xv[:, t0 : t0 + T, :],
             )
             x_sb[b] = xt
-            kt = sb.tile([P, 4 * E], BF16, name="k_sb", tag="k_sb", bufs=6)
+            kt = sb.tile([P, 8 * E], BF16, name="k_sb", tag="k_sb", bufs=3)
             k3 = kt[:, 0 : E * T].rearrange("p (h e) -> p h e", e=E)
             rows = kv[16 * t0 : 16 * (t0 + T), :, :].rearrange("r (h l) e -> l r h e", l=L)
             for l in range(L):
@@ -127,12 +128,11 @@ def tile_dividedspacetimeattention_pa_t_kernel(tc, x, Wq, bq, k, out):
         def size(b):
             return BLOCKS[b][1]
 
-        def split(b):
-            return SPLIT[2] if size(b) == 2 else SPLIT[40 + b % 2]
+        def split(i):
+            b, g0, ng = HALVES[i]
+            return (g0, ng - 1), g0 + ng - 1
 
         def tp(b, w, m):
-            if m >= size(b) // 2:
-                return
             tr = ps.tile([P, 512], F32, name="tr", tag="tr", bufs=4)
             src = (x_sb if w == "x" else k_sb)[b][:].bitcast(F32)
             trv = tr[:].rearrange("p (u c s f) -> p u c s f", u=2, c=8, s=2, f=16)
@@ -149,11 +149,9 @@ def tile_dividedspacetimeattention_pa_t_kernel(tc, x, Wq, bq, k, out):
 
         def cp(b, w, m):
             T = size(b)
-            if m >= T // 2:
-                return
             if w == "x":
                 if m == 0:
-                    xg[b] = sb.tile([P, 4 * E], BF16, name="xg", tag="xg", bufs=3, align_bytes=64)
+                    xg[b] = sb.tile([P, 8 * E], BF16, name="xg", tag="xg", bufs=2, align_bytes=64)
                 gv = xg[b][:].bitcast(F32)[:, 0 : 256 * T].rearrange(
                     "p (c m q u) -> p c m q u", c=8, m=T // 2, q=32, u=2
                 )
@@ -163,7 +161,7 @@ def tile_dividedspacetimeattention_pa_t_kernel(tc, x, Wq, bq, k, out):
                 )
             else:
                 if m == 0:
-                    kg[b] = sb.tile([P, 4 * E], BF16, name="kg", tag="kg", bufs=3, align_bytes=64)
+                    kg[b] = sb.tile([P, 8 * E], BF16, name="kg", tag="kg", bufs=2, align_bytes=64)
                 nc.scalar.copy(
                     out=kg[b][:].bitcast(F32)[:, 512 * m : 512 * m + 512].rearrange(
                         "p (s q u) -> p s q u", s=2, q=P, u=2
@@ -171,101 +169,109 @@ def tile_dividedspacetimeattention_pa_t_kernel(tc, x, Wq, bq, k, out):
                     in_=tr_of[(w, b, m)][:].rearrange("p (s u q) -> p s q u", s=2, u=2, q=P),
                 )
 
-        def quant(src, b, store, tag, bufs):
-            T = size(b)
+        def quant(src, i, store, tag, bufs):
+            b, g0, ng = HALVES[i]
             c = sb.tile([P, 512], U32, name=tag + "c", tag=tag + "c", bufs=bufs, align_bytes=64)
             s = sb.tile([P, 512], U8, name=tag + "s", tag=tag + "s", bufs=bufs, align_bytes=64)
             nc.vector.quantize_mx(
-                out=c[:, 0 : P * T].bitcast(FP8X4), scales=s[:, 0 : P * T], in_=src[b][:, 0 : E * T]
+                out=c[:, 0 : P * ng].bitcast(FP8X4),
+                scales=s[:, 0 : P * ng],
+                in_=src[:, 0 : E * ng],
             )
-            store[b] = (c, s)
+            store[i] = (c, s)
 
-        def m1_pass(b, y, o, j, g0, n):
-            c, s = xc[b]
+        def qx(i):
+            b, g0, ng = HALVES[i]
+            quant(xg[b][:, E * g0 : E * (g0 + ng)], i, xc, "x", 2)
+
+        def qk(i):
+            b, g0, ng = HALVES[i]
+            quant(kg[b][:, E * g0 : E * (g0 + ng)], i, kc, "k", 4)
+
+        def qq(i):
+            quant(qg[i], i, qc, "q", 3)
+
+        def m1_pass(i, y, o, j, g, n):
+            c, s = xc[i]
+            o0 = P * (g - HALVES[i][1])
             nc.tensor.matmul_mx(
                 out=y[:, o : o + n],
                 lhsT=wc[:, P * j : P * j + P].bitcast(FP8X4),
                 lhsT_scale=ws[:, P * j : P * j + P],
-                rhs=c[:, P * g0 : P * g0 + n].bitcast(FP8X4),
-                rhs_scale=s[:, P * g0 : P * g0 + n],
+                rhs=c[:, o0 : o0 + n].bitcast(FP8X4),
+                rhs_scale=s[:, o0 : o0 + n],
                 start=True,
                 stop=True,
             )
 
-        def m1s(b, i):
-            g0, ng = split(b)[0]
+        def per_bank(i):
+            return 4 // split(i)[0][1] if split(i)[0][1] < 3 else 1
+
+        def m1s(i, u):
+            (g0, ng), gv = split(i)
             n = P * ng
-            per = {1: 4, 2: 2, 3: 1, 4: 1}[ng]
-            if per * i >= 4:
+            per = per_bank(i)
+            if per * u >= 4:
                 return
             y = ps.tile([P, 512], F32, name="y", tag="y", bufs=3)
-            for j in range(per * i, per * i + per):
-                for lo, ln in {1: ((0, 1),), 2: ((0, 2),), 3: ((0, 2), (2, 1)), 4: ((0, 4),)}[ng]:
-                    m1_pass(b, y, n * (j % per) + P * lo, j, g0 + lo, P * ln)
-            y_of[(b, i)] = y
+            for j in range(per * u, per * u + per):
+                o = n * (j % per)
+                lo = 0
+                for ln in (2, 1):
+                    if lo + ln <= ng:
+                        m1_pass(i, y, o + P * lo, j, g0 + lo, P * ln)
+                        lo += ln
+            y_of[(i, u)] = y
 
-        def act(b, i):
-            g0, ng = split(b)[0]
+        def act(i, u):
+            (g0, ng), gv = split(i)
             n = P * ng
-            per = {1: 4, 2: 2, 3: 1, 4: 1}[ng]
-            if per * i >= 4:
+            per = per_bank(i)
+            if per * u >= 4:
                 return
-            if i == 0:
-                qp[b] = sb.tile([P, 4, n], BF16, name="qp%d" % ng, tag="qp%d" % ng, bufs=2)
-            for j in range(per * i, per * i + per):
+            if u == 0:
+                qp[i] = sb.tile([P, 4, n], BF16, name="qp%d" % ng, tag="qp%d" % ng, bufs=2)
+            for j in range(per * u, per * u + per):
                 o = n * (j % per)
                 nc.scalar.activation(
-                    out=qp[b][:, j, :],
-                    in_=y_of[(b, i)][:, o : o + n],
+                    out=qp[i][:, j, :],
+                    in_=y_of[(i, u)][:, o : o + n],
                     func=ACT.Identity,
                     bias=b32[:, j : j + 1],
                     scale=1.0,
                 )
 
-        def new_q(b):
-            qg[b] = sb.tile([P, 4 * E], BF16, name="qg", tag="qg", bufs=3, align_bytes=64)
+        def new_q(i):
+            qg[i] = sb.tile([P, 4 * E], BF16, name="qg", tag="qg", bufs=3, align_bytes=64)
 
-        def rg(b):
-            g0, ng = split(b)[0]
+        def rg(i):
+            (g0, ng), gv = split(i)
             nc.vector.tensor_copy(
-                out=qg[b][:, E * g0 : E * (g0 + ng)].rearrange("p (c i j) -> p c j i", i=4, j=4),
-                in_=qp[b][:].rearrange("p j (c i) -> p c j i", i=4),
+                out=qg[i][:, 0 : E * ng].rearrange("p (c i j) -> p c j i", i=4, j=4),
+                in_=qp[i][:].rearrange("p j (c i) -> p c j i", i=4),
             )
 
-        def m1v(b, i):
-            if i >= len(split(b)[1]):
-                return
+        def m1v(i):
             y = ps.tile([P, 512], F32, name="y", tag="y", bufs=3)
             for j in range(4):
-                m1_pass(b, y, P * j, j, split(b)[1][i], P)
-            y_of[(b, 4 + i)] = y
+                m1_pass(i, y, P * j, j, split(i)[1], P)
+            y_of[(i, 4)] = y
 
-        def vd(b, i):
-            if i >= len(split(b)[1]):
-                return
-            g = split(b)[1][i]
+        def vd(i):
+            o = E * (HALVES[i][2] - 1)
             nc.vector.tensor_tensor(
-                out=qg[b][:, E * g : E * g + E].rearrange("p (q j) -> p q j", j=4),
-                in0=y_of[(b, 4 + i)][:].rearrange("p (j q) -> p q j", j=4),
+                out=qg[i][:, o : o + E].rearrange("p (q j) -> p q j", j=4),
+                in0=y_of[(i, 4)][:].rearrange("p (j q) -> p q j", j=4),
                 in1=b32[:].unsqueeze(1).to_broadcast([P, P, 4]),
                 op=ALU.add,
             )
 
-        def qq(b):
-            T = size(b)
-            c = sb.tile([P, 512], U32, name="qc", tag="qc", bufs=3, align_bytes=64)
-            s = sb.tile([P, 512], U8, name="qs", tag="qs", bufs=3, align_bytes=64)
-            nc.vector.quantize_mx(
-                out=c[:, 0 : P * T].bitcast(FP8X4), scales=s[:, 0 : P * T], in_=qg[b][:, 0 : E * T]
-            )
-            qc[b] = (c, s)
-
-        def m2(b):
-            c, s = qc[b]
-            c2, s2 = kc[b]
+        def m2(i):
+            c, s = qc[i]
+            c2, s2 = kc[i]
             sc = ps.tile([P, 512], F32, name="sc", tag="sc", bufs=1)
-            sc_of[b] = sc
-            for g in range(size(b)):
+            sc_of[i] = sc
+            for g in range(HALVES[i][2]):
                 nc.tensor.matmul_mx(
                     out=sc[:, P * g : P * g + P],
                     lhsT=c[:, P * g : P * g + P].bitcast(FP8X4),
@@ -285,131 +291,123 @@ def tile_dividedspacetimeattention_pa_t_kernel(tc, x, Wq, bq, k, out):
                     stop=True,
                 )
 
-        def pair(b):
-            return (b + 1) // 2, 0 if b % 2 else 16 * size(b - 1) if b else 0
-
-        def width(p):
-            return 16 * sum(size(b) for b in range(nb) if pair(b)[0] == p)
-
-        def red(b):
-            p, c0 = pair(b)
-            if p not in s_sb:
-                s_sb[p] = sb.tile([P, 128], F32, name="s_sb", tag="s_sb", bufs=3)
-            w = size(b)
+        def red(i):
+            b, g0, ng = HALVES[i]
+            if g0 == 0:
+                s_sb[b] = sb.tile([P, 128], F32, name="s_sb", tag="s_sb", bufs=3)
             nc.vector.tensor_reduce(
-                out=s_sb[p][:, c0 : c0 + 16 * w].rearrange("p (l g) -> p l g", g=16),
-                in_=sc_of[b][:, 0 : P * w].rearrange("p (l t g) -> p l g t", t=8, g=16),
+                out=s_sb[b][:, 16 * g0 : 16 * (g0 + ng)].rearrange("p (l g) -> p l g", g=16),
+                in_=sc_of[i][:, 0 : P * ng].rearrange("p (l t g) -> p l g t", t=8, g=16),
                 axis=AX.X,
                 op=ALU.max,
             )
 
         def vec(t, n):
-            return t[:, 0:n].rearrange("p (l g) -> p l g", g=16)
+            return t[:, 0 : 16 * n].rearrange("p (l g) -> p l g", g=16)
 
-        def smax(p):
-            n = width(p)
+        def smax(b):
+            T = size(b)
             mx = sb.tile([P, 8], F32, name="mx", tag="mx", bufs=2)
-            nc.vector.tensor_reduce(out=mx[:, 0 : n // 16], in_=vec(s_sb[p], n), axis=AX.X, op=ALU.max)
-            mx_sb[p] = mx
+            nc.vector.tensor_reduce(out=mx[:, 0:T], in_=vec(s_sb[b], T), axis=AX.X, op=ALU.max)
+            mx_sb[b] = mx
 
-        def sub(p):
-            n = width(p)
+        def sub(b):
+            T = size(b)
             d = sb.tile([P, 128], F32, name="d_sb", tag="d_sb", bufs=2)
             nc.gpsimd.tensor_tensor(
-                out=vec(d, n),
-                in0=vec(s_sb[p], n),
-                in1=mx_sb[p][:, 0 : n // 16].unsqueeze(2).to_broadcast([P, n // 16, 16]),
+                out=vec(d, T),
+                in0=vec(s_sb[b], T),
+                in1=mx_sb[b][:, 0:T].unsqueeze(2).to_broadcast([P, T, 16]),
                 op=ALU.subtract,
             )
-            d_sb[p] = d
+            d_sb[b] = d
 
-        def expo(p):
-            n = width(p)
+        def expo(b):
+            n = 16 * size(b)
             ex = sb.tile([P, 128], F32, name="e_sb", tag="e_sb", bufs=2)
-            nc.scalar.activation(out=ex[:, 0:n], in_=d_sb[p][:, 0:n], func=ACT.Exp, scale=0.125)
-            e_sb[p] = ex
+            nc.scalar.activation(out=ex[:, 0:n], in_=d_sb[b][:, 0:n], func=ACT.Exp, scale=0.125)
+            e_sb[b] = ex
 
-        def ssum(p):
-            n = width(p)
+        def ssum(b):
+            T = size(b)
             z = sb.tile([P, 8], F32, name="z", tag="z", bufs=2)
-            nc.vector.tensor_reduce(out=z[:, 0 : n // 16], in_=vec(e_sb[p], n), axis=AX.X, op=ALU.add)
-            r_sb[p] = z
+            nc.vector.tensor_reduce(out=z[:, 0:T], in_=vec(e_sb[b], T), axis=AX.X, op=ALU.add)
+            r_sb[b] = z
 
-        def recip(p):
-            n = width(p)
+        def recip(b):
+            T = size(b)
             r = sb.tile([P, 8], F32, name="r", tag="r", bufs=2)
-            nc.vector.reciprocal(out=r[:, 0 : n // 16], in_=r_sb[p][:, 0 : n // 16])
-            r_sb[p] = r
+            nc.vector.reciprocal(out=r[:, 0:T], in_=r_sb[b][:, 0:T])
+            r_sb[b] = r
 
-        def finish(p):
-            n = width(p)
+        def finish(b):
+            t0, T = BLOCKS[b]
+            L = 8 // T
             o = sb.tile([P, 128], F32, name="o_sb", tag="o_sb", bufs=3)
             nc.gpsimd.tensor_tensor(
-                out=vec(o, n),
-                in0=vec(e_sb[p], n),
-                in1=r_sb[p][:, 0 : n // 16].unsqueeze(2).to_broadcast([P, n // 16, 16]),
+                out=vec(o, T),
+                in0=vec(e_sb[b], T),
+                in1=r_sb[b][:, 0:T].unsqueeze(2).to_broadcast([P, T, 16]),
                 op=ALU.mult,
             )
-            for b in range(nb):
-                if pair(b)[0] == p:
-                    t0, T = BLOCKS[b]
-                    L = 8 // T
-                    c0 = pair(b)[1]
-                    o3 = vec(o, n)[:, c0 // 16 : c0 // 16 + T, :]
-                    rows = ov[16 * t0 : 16 * (t0 + T), :, :].rearrange("r (h l) g -> l r h g", l=L)
-                    for l in range(L):
-                        nc.sync.dma_start(out=rows[l], in_=o3[16 * T * l : 16 * T * (l + 1), :, :])
+            rows = ov[16 * t0 : 16 * (t0 + T), :, :].rearrange("r (h l) g -> l r h g", l=L)
+            for l in range(L):
+                nc.sync.dma_start(out=rows[l], in_=vec(o, T)[16 * T * l : 16 * T * (l + 1), :, :])
 
-        def on(f, b, *args):
-            if 0 <= b < nb:
-                f(b, *args)
+        def on(f, i, *args):
+            if 0 <= i < nh:
+                f(i, *args)
 
-        def onp(f, b):
-            if 0 <= b < nb and (b + 1 == nb or pair(b + 1)[0] != pair(b)[0]):
-                f(pair(b)[0])
+        def onb(f, i):
+            if 0 <= i < nh and HALVES[i][1] + HALVES[i][2] == size(HALVES[i][0]):
+                f(HALVES[i][0])
+
+        def turns(i):
+            if i >= nh or HALVES[i][0] + 1 == nb:
+                return []
+            b, g0, ng = HALVES[i]
+            todo = [(b + 1, w, m) for w in ("x", "k") for m in range(size(b + 1) // 2)]
+            if size(b) < 8:
+                return todo
+            cut = len(todo) // 2
+            return todo[cut:] if g0 else todo[:cut]
 
         for w in ("x", "k"):
-            for m in range(2):
-                tp(0, w, m)
-            for m in range(2):
-                cp(0, w, m)
-        quant(xg, 0, xc, "x", 2)
+            tp(0, w, 0)
+            cp(0, w, 0)
+        qx(0)
 
-        for n in range(nb + 5):
-            on(load, n + 3)
-            on(tp, n + 1, "x", 0)
-            on(tp, n + 1, "x", 1)
-            on(tp, n + 1, "k", 0)
-            on(tp, n + 1, "k", 1)
-            on(cp, n + 1, "x", 0)
-            on(cp, n + 1, "x", 1)
-            on(cp, n + 1, "k", 0)
-            on(cp, n + 1, "k", 1)
-            if n < nb:
-                new_q(n)
-            on(m1v, n, 0)
-            if n < nb:
-                quant(kg, n, kc, "k", 4)
-            on(red, n - 3)
-            on(rg, n - 1)
-            onp(smax, n - 3)
-            onp(ssum, n - 5)
-            on(vd, n, 0)
-            if n + 1 < nb:
-                quant(xg, n + 1, xc, "x", 2)
-            if 0 < n <= nb:
-                qq(n - 1)
-            onp(sub, n - 3)
-            onp(recip, n - 5)
-            onp(finish, n - 5)
-
-            on(m1s, n, 0)
-            on(m1s, n, 1)
-            on(act, n, 0)
-            on(m2, n - 2)
-            on(m1s, n, 2)
-            on(act, n, 1)
-            on(m1s, n, 3)
-            on(act, n, 2)
-            on(act, n, 3)
-            onp(expo, n - 4)
+        for i in range(nh + 5):
+            if i < nh and HALVES[i][1] == 0 and HALVES[i][0] + 3 < nb:
+                load(HALVES[i][0] + 3)
+            todo = turns(i)
+            first = todo[: (len(todo) + 1) // 2]
+            for t in first:
+                tp(*t)
+                cp(*t)
+            on(new_q, i)
+            on(m1v, i)
+            on(qk, i)
+            on(red, i - 3)
+            on(rg, i - 1)
+            onb(smax, i - 3)
+            onb(ssum, i - 5)
+            on(vd, i)
+            on(qx, i + 1)
+            on(qq, i - 1)
+            onb(sub, i - 3)
+            onb(recip, i - 5)
+            onb(finish, i - 5)
+            on(m1s, i, 0)
+            on(m1s, i, 1)
+            on(act, i, 0)
+            on(act, i, 1)
+            for t in todo[len(first) :]:
+                tp(*t)
+                cp(*t)
+            on(m2, i - 2)
+            on(m1s, i, 2)
+            on(m1s, i, 3)
+            on(act, i, 2)
+            on(act, i, 3)
+            onb(expo, i - 4)

@@ -19,7 +19,7 @@ FLOPS = 2 * 12544 * 512 * 512 + 2 * 784 * 16 * 16 * 512
 BIG = 2.0 ** 100
 
 
-BLOCKS = [(0, 2), (2, 4)] + [(6 + 8 * i, 8) for i in range(11)] + [(94, 4)]
+BLOCKS = [(8 * i, 8) for i in range(12)] + [(96, 2)]
 
 
 def tile_dividedspacetimeattention_pa_t_kernel(tc, x, Wq, bq, k, out):
@@ -55,15 +55,23 @@ def tile_dividedspacetimeattention_pa_t_kernel(tc, x, Wq, bq, k, out):
         y_of = {}
         sc_of = {}
 
-        def load(b):
+        def size(b):
+            return BLOCKS[b][1]
+
+        def load_x(b, pieces):
+            t0, T = BLOCKS[b]
+            xt = sb.tile([P, 8 * E], BF16, name="x_sb", tag="x_sb", bufs=3)
+            n = T // pieces
+            for a in range(0, T, n):
+                nc.sync.dma_start(
+                    out=xt[:, E * a : E * (a + n)].rearrange("p (t e) -> p t e", e=E),
+                    in_=xv[:, t0 + a : t0 + a + n, :],
+                )
+            x_sb[b] = xt
+
+        def load_k(b):
             t0, T = BLOCKS[b]
             L = 8 // T
-            xt = sb.tile([P, 8 * E], BF16, name="x_sb", tag="x_sb", bufs=3)
-            nc.sync.dma_start(
-                out=xt[:, 0 : E * T].rearrange("p (t e) -> p t e", e=E),
-                in_=xv[:, t0 : t0 + T, :],
-            )
-            x_sb[b] = xt
             kt = sb.tile([P, 8 * E], BF16, name="k_sb", tag="k_sb", bufs=3)
             k3 = kt[:, 0 : E * T].rearrange("p (h e) -> p h e", e=E)
             rows = kv[16 * t0 : 16 * (t0 + T), :, :].rearrange("r (h l) e -> l r h e", l=L)
@@ -71,13 +79,15 @@ def tile_dividedspacetimeattention_pa_t_kernel(tc, x, Wq, bq, k, out):
                 nc.sync.dma_start(out=k3[16 * T * l : 16 * T * (l + 1), :, :], in_=rows[l])
             k_sb[b] = kt
 
-        load(0)
         wraw = const.tile([P, 4, E], BF16, name="wraw")
         nc.sync.dma_start(out=wraw[:], in_=Wq.rearrange("(p j) n -> p j n", j=4))
         b_bf = const.tile([P, 4], BF16, name="b_bf")
         nc.scalar.dma_start(out=b_bf[:], in_=bq.rearrange("(p j) -> p j", j=4))
-        load(1)
-        load(2)
+        load_x(0, size(0) // 2)
+        load_x(1, 4)
+        load_k(0)
+        load_x(2, 1)
+        load_k(1)
 
         ident = const.tile([P, P], F32, name="ident")
         make_identity(nc, ident[:])
@@ -92,16 +102,17 @@ def tile_dividedspacetimeattention_pa_t_kernel(tc, x, Wq, bq, k, out):
             in_=ident[:].rearrange("p (b f j) -> p b j f", b=4, f=16, j=2),
         )
         ag = const.tile([P, 4 * P], BF16, name="ag", align_bytes=64)
-        bg = const.tile([P, 4 * P], BF16, name="bg", align_bytes=64)
-        nc.vector.memset(ag[:], 0.0)
-        nc.vector.memset(bg[:], 0.0)
+        bg = const.tile([P, 16 * P], BF16, name="bg", align_bytes=64)
+        nc.gpsimd.memset(ag[:], 0.0)
+        nc.gpsimd.memset(bg[:], 0.0)
+        slot4 = ident[:, 0:8].unsqueeze(1).unsqueeze(3).to_broadcast([P, 4, 8, 16])
         slot = ident[:, 0:8].unsqueeze(2).to_broadcast([P, 8, 16])
         nc.vector.tensor_copy(
             out=ag[:].rearrange("p (s f j) -> p s f j", s=8, f=16, j=4)[:, :, :, 0], in_=slot
         )
         nc.vector.tensor_scalar(
-            out=bg[:].rearrange("p (s f j) -> p s f j", s=8, f=16, j=4)[:, :, :, 0],
-            in0=slot,
+            out=bg[:].rearrange("p (l s f j) -> p l s f j", l=4, s=8, f=16, j=4)[:, :, :, :, 0],
+            in0=slot4,
             scalar1=-1.0,
             scalar2=BIG,
             op0=ALU.add,
@@ -109,8 +120,8 @@ def tile_dividedspacetimeattention_pa_t_kernel(tc, x, Wq, bq, k, out):
         )
         ac = const.tile([P, P], U32, name="ac", align_bytes=64)
         asc = const.tile([P, P], U8, name="asc", align_bytes=64)
-        bc = const.tile([P, P], U32, name="bc", align_bytes=64)
-        bsc = const.tile([P, P], U8, name="bsc", align_bytes=64)
+        bc = const.tile([P, 4 * P], U32, name="bc", align_bytes=64)
+        bsc = const.tile([P, 4 * P], U8, name="bsc", align_bytes=64)
         nc.vector.quantize_mx(out=ac[:].bitcast(FP8X4), scales=asc[:], in_=ag[:])
         nc.vector.quantize_mx(out=bc[:].bitcast(FP8X4), scales=bsc[:], in_=bg[:])
 
@@ -125,12 +136,10 @@ def tile_dividedspacetimeattention_pa_t_kernel(tc, x, Wq, bq, k, out):
         ws = const.tile([P, E], U8, name="ws", align_bytes=64)
         nc.vector.quantize_mx(out=wc[:].bitcast(FP8X4), scales=ws[:], in_=wg[:])
 
-        def size(b):
-            return BLOCKS[b][1]
-
         def split(i):
             b, g0, ng = HALVES[i]
-            return (g0, ng - 1), g0 + ng - 1
+            n = ng - 1
+            return (g0, n), range(g0 + n, g0 + ng)
 
         def tp(b, w, m):
             tr = ps.tile([P, 512], F32, name="tr", tag="tr", bufs=4)
@@ -151,7 +160,7 @@ def tile_dividedspacetimeattention_pa_t_kernel(tc, x, Wq, bq, k, out):
             T = size(b)
             if w == "x":
                 if m == 0:
-                    xg[b] = sb.tile([P, 8 * E], BF16, name="xg", tag="xg", bufs=2, align_bytes=64)
+                    xg[b] = sb.tile([P, 8 * E], BF16, name="xg", tag="xg", bufs=3, align_bytes=64)
                 gv = xg[b][:].bitcast(F32)[:, 0 : 256 * T].rearrange(
                     "p (c m q u) -> p c m q u", c=8, m=T // 2, q=32, u=2
                 )
@@ -161,7 +170,7 @@ def tile_dividedspacetimeattention_pa_t_kernel(tc, x, Wq, bq, k, out):
                 )
             else:
                 if m == 0:
-                    kg[b] = sb.tile([P, 8 * E], BF16, name="kg", tag="kg", bufs=2, align_bytes=64)
+                    kg[b] = sb.tile([P, 8 * E], BF16, name="kg", tag="kg", bufs=3, align_bytes=64)
                 nc.scalar.copy(
                     out=kg[b][:].bitcast(F32)[:, 512 * m : 512 * m + 512].rearrange(
                         "p (s q u) -> p s q u", s=2, q=P, u=2
@@ -205,7 +214,7 @@ def tile_dividedspacetimeattention_pa_t_kernel(tc, x, Wq, bq, k, out):
             )
 
         def per_bank(i):
-            return 4 // split(i)[0][1] if split(i)[0][1] < 3 else 1
+            return {1: 4, 2: 2, 3: 1, 4: 1}[split(i)[0][1]]
 
         def m1s(i, u):
             (g0, ng), gv = split(i)
@@ -217,7 +226,7 @@ def tile_dividedspacetimeattention_pa_t_kernel(tc, x, Wq, bq, k, out):
             for j in range(per * u, per * u + per):
                 o = n * (j % per)
                 lo = 0
-                for ln in (2, 1):
+                for ln in (4, 2, 1):
                     if lo + ln <= ng:
                         m1_pass(i, y, o + P * lo, j, g0 + lo, P * ln)
                         lo += ln
@@ -251,17 +260,21 @@ def tile_dividedspacetimeattention_pa_t_kernel(tc, x, Wq, bq, k, out):
                 in_=qp[i][:].rearrange("p j (c i) -> p c j i", i=4),
             )
 
-        def m1v(i):
+        def m1v(i, v):
+            if v >= len(split(i)[1]):
+                return
             y = ps.tile([P, 512], F32, name="y", tag="y", bufs=3)
             for j in range(4):
-                m1_pass(i, y, P * j, j, split(i)[1], P)
-            y_of[(i, 4)] = y
+                m1_pass(i, y, P * j, j, split(i)[1][v], P)
+            y_of[(i, 4 + v)] = y
 
-        def vd(i):
-            o = E * (HALVES[i][2] - 1)
+        def vd(i, v):
+            if v >= len(split(i)[1]):
+                return
+            o = E * (split(i)[1][v] - HALVES[i][1])
             nc.vector.tensor_tensor(
                 out=qg[i][:, o : o + E].rearrange("p (q j) -> p q j", j=4),
-                in0=y_of[(i, 4)][:].rearrange("p (j q) -> p q j", j=4),
+                in0=y_of[(i, 4 + v)][:].rearrange("p (j q) -> p q j", j=4),
                 in1=b32[:].unsqueeze(1).to_broadcast([P, P, 4]),
                 op=ALU.add,
             )
@@ -271,24 +284,25 @@ def tile_dividedspacetimeattention_pa_t_kernel(tc, x, Wq, bq, k, out):
             c2, s2 = kc[i]
             sc = ps.tile([P, 512], F32, name="sc", tag="sc", bufs=1)
             sc_of[i] = sc
-            for g in range(HALVES[i][2]):
+            ng = HALVES[i][2]
+            nc.tensor.matmul_mx(
+                out=sc[:, 0 : P * ng],
+                lhsT=ac[:].bitcast(FP8X4),
+                lhsT_scale=asc[:],
+                rhs=bc[:, 0 : P * ng].bitcast(FP8X4),
+                rhs_scale=bsc[:, 0 : P * ng],
+                start=True,
+                stop=False,
+            )
+            for g in range(ng):
                 nc.tensor.matmul_mx(
                     out=sc[:, P * g : P * g + P],
                     lhsT=c[:, P * g : P * g + P].bitcast(FP8X4),
                     lhsT_scale=s[:, P * g : P * g + P],
                     rhs=c2[:, P * g : P * g + P].bitcast(FP8X4),
                     rhs_scale=s2[:, P * g : P * g + P],
-                    start=True,
-                    stop=False,
-                )
-                nc.tensor.matmul_mx(
-                    out=sc[:, P * g : P * g + P],
-                    lhsT=ac[:].bitcast(FP8X4),
-                    lhsT_scale=asc[:],
-                    rhs=bc[:].bitcast(FP8X4),
-                    rhs_scale=bsc[:],
                     start=False,
-                    stop=True,
+                    stop=g == ng - 1,
                 )
 
         def red(i):
@@ -363,51 +377,59 @@ def tile_dividedspacetimeattention_pa_t_kernel(tc, x, Wq, bq, k, out):
                 f(HALVES[i][0])
 
         def turns(i):
-            if i >= nh or HALVES[i][0] + 1 == nb:
+            if i >= nh:
                 return []
             b, g0, ng = HALVES[i]
-            todo = [(b + 1, w, m) for w in ("x", "k") for m in range(size(b + 1) // 2)]
-            if size(b) < 8:
-                return todo
-            cut = len(todo) // 2
-            return todo[cut:] if g0 else todo[:cut]
+            todo = []
+            if g0 == 0 and b + 1 < nb:
+                todo += [(b + 1, "x", m) for m in range(size(b + 1) // 2)]
+            if g0 + ng == size(b):
+                todo += [(b, "k", m) for m in range(size(b) // 2)]
+            return todo
 
-        for w in ("x", "k"):
-            tp(0, w, 0)
-            cp(0, w, 0)
+        for m in range(size(0) // 2):
+            tp(0, "x", m)
+            cp(0, "x", m)
         qx(0)
 
-        for i in range(nh + 5):
-            if i < nh and HALVES[i][1] == 0 and HALVES[i][0] + 3 < nb:
-                load(HALVES[i][0] + 3)
-            todo = turns(i)
-            first = todo[: (len(todo) + 1) // 2]
-            for t in first:
-                tp(*t)
-                cp(*t)
+        for i in range(-1, nh + 8):
+            todo = turns(i + 1)
+            first = todo[: len(todo) // 2]
             on(new_q, i)
-            on(m1v, i)
-            on(qk, i)
-            on(red, i - 3)
-            on(rg, i - 1)
-            onb(smax, i - 3)
-            onb(ssum, i - 5)
-            on(vd, i)
-            on(qx, i + 1)
-            on(qq, i - 1)
-            onb(sub, i - 3)
-            onb(recip, i - 5)
-            onb(finish, i - 5)
+            on(m1v, i, 0)
             on(m1s, i, 0)
             on(m1s, i, 1)
             on(act, i, 0)
             on(act, i, 1)
-            for t in todo[len(first) :]:
+            for t in first:
                 tp(*t)
                 cp(*t)
+            onb(smax, i - 3)
+            on(vd, i, 0)
+            onb(sub, i - 3)
+            on(qk, i - 1)
             on(m2, i - 2)
             on(m1s, i, 2)
+            on(m1v, i, 1)
             on(m1s, i, 3)
             on(act, i, 2)
             on(act, i, 3)
+            on(vd, i, 1)
+            on(qq, i - 1)
+            if i >= 0:
+                on(qx, i + 1)
+            onb(recip, i - 6)
+            on(red, i - 2)
+            onb(finish, i - 6)
+            onb(ssum, i - 5)
+            on(rg, i)
+            for t in todo[len(first) :]:
+                tp(*t)
+                cp(*t)
             onb(expo, i - 4)
+            if 0 <= i + 1 < nh:
+                b, g0, ng = HALVES[i + 1]
+                if g0 == 0 and b + 3 < nb:
+                    load_x(b + 3, 1)
+                if g0 + ng == size(b) and b + 2 < nb:
+                    load_k(b + 2)

@@ -84,10 +84,11 @@ def tile_dividedspacetimeattention_pa_t_kernel(tc, x, Wq, bq, k, out):
         b_bf = const.tile([P, 4], BF16, name="b_bf")
         nc.scalar.dma_start(out=b_bf[:], in_=bq.rearrange("(p j) -> p j", j=4))
         load_x(0, size(0) // 2)
-        load_x(1, 4)
+        load_x(1, 2)
         load_k(0)
         load_x(2, 1)
         load_k(1)
+        load_k(2)
 
         ident = const.tile([P, P], F32, name="ident")
         make_identity(nc, ident[:])
@@ -138,7 +139,7 @@ def tile_dividedspacetimeattention_pa_t_kernel(tc, x, Wq, bq, k, out):
 
         def split(i):
             b, g0, ng = HALVES[i]
-            n = ng - 1
+            n = ng if i == nh - 1 else ng - 1
             return (g0, n), range(g0 + n, g0 + ng)
 
         def tp(b, w, m):
@@ -392,8 +393,8 @@ def tile_dividedspacetimeattention_pa_t_kernel(tc, x, Wq, bq, k, out):
             cp(0, "x", m)
         qx(0)
 
-        for i in range(-1, nh + 8):
-            todo = turns(i + 1)
+        for i in range(nh + 8):
+            todo = turns(i)
             first = todo[: len(todo) // 2]
             on(new_q, i)
             on(m1v, i, 0)
@@ -407,7 +408,7 @@ def tile_dividedspacetimeattention_pa_t_kernel(tc, x, Wq, bq, k, out):
             onb(smax, i - 3)
             on(vd, i, 0)
             onb(sub, i - 3)
-            on(qk, i - 1)
+            on(qq, i - 1)
             on(m2, i - 2)
             on(m1s, i, 2)
             on(m1v, i, 1)
@@ -415,21 +416,20 @@ def tile_dividedspacetimeattention_pa_t_kernel(tc, x, Wq, bq, k, out):
             on(act, i, 2)
             on(act, i, 3)
             on(vd, i, 1)
-            on(qq, i - 1)
-            if i >= 0:
-                on(qx, i + 1)
+            on(qx, i + 1)
             onb(recip, i - 6)
             on(red, i - 2)
             onb(finish, i - 6)
+            on(qk, i - 1)
             onb(ssum, i - 5)
             on(rg, i)
             for t in todo[len(first) :]:
                 tp(*t)
                 cp(*t)
             onb(expo, i - 4)
-            if 0 <= i + 1 < nh:
-                b, g0, ng = HALVES[i + 1]
+            if i < nh:
+                b, g0, ng = HALVES[i]
                 if g0 == 0 and b + 3 < nb:
                     load_x(b + 3, 1)
-                if g0 + ng == size(b) and b + 2 < nb:
-                    load_k(b + 2)
+                if g0 + ng == size(b) and b + 3 < nb:
+                    load_k(b + 3)

@@ -16,8 +16,9 @@ P = 128
 E = 512
 STEPS = 98
 FLOPS = 2 * 12544 * 512 * 512 + 2 * 784 * 16 * 16 * 512
-BIG = 2.0 ** 100
 
+
+BIG = 2.0 ** 100
 
 BLOCKS = [(8 * i, 8) for i in range(12)] + [(96, 2)]
 
@@ -46,6 +47,7 @@ def tile_dividedspacetimeattention_pa_t_kernel(tc, x, Wq, bq, k, out):
         qp = {}
         qg = {}
         qc = {}
+        raw = {}
         s_sb = {}
         d_sb = {}
         e_sb = {}
@@ -103,17 +105,16 @@ def tile_dividedspacetimeattention_pa_t_kernel(tc, x, Wq, bq, k, out):
             in_=ident[:].rearrange("p (b f j) -> p b j f", b=4, f=16, j=2),
         )
         ag = const.tile([P, 4 * P], BF16, name="ag", align_bytes=64)
-        bg = const.tile([P, 16 * P], BF16, name="bg", align_bytes=64)
+        bg = const.tile([P, 4 * P], BF16, name="bg", align_bytes=64)
         nc.gpsimd.memset(ag[:], 0.0)
         nc.gpsimd.memset(bg[:], 0.0)
-        slot4 = ident[:, 0:8].unsqueeze(1).unsqueeze(3).to_broadcast([P, 4, 8, 16])
         slot = ident[:, 0:8].unsqueeze(2).to_broadcast([P, 8, 16])
         nc.vector.tensor_copy(
             out=ag[:].rearrange("p (s f j) -> p s f j", s=8, f=16, j=4)[:, :, :, 0], in_=slot
         )
         nc.vector.tensor_scalar(
-            out=bg[:].rearrange("p (l s f j) -> p l s f j", l=4, s=8, f=16, j=4)[:, :, :, :, 0],
-            in0=slot4,
+            out=bg[:].rearrange("p (s f j) -> p s f j", s=8, f=16, j=4)[:, :, :, 0],
+            in0=slot,
             scalar1=-1.0,
             scalar2=BIG,
             op0=ALU.add,
@@ -121,8 +122,8 @@ def tile_dividedspacetimeattention_pa_t_kernel(tc, x, Wq, bq, k, out):
         )
         ac = const.tile([P, P], U32, name="ac", align_bytes=64)
         asc = const.tile([P, P], U8, name="asc", align_bytes=64)
-        bc = const.tile([P, 4 * P], U32, name="bc", align_bytes=64)
-        bsc = const.tile([P, 4 * P], U8, name="bsc", align_bytes=64)
+        bc = const.tile([P, P], U32, name="bc", align_bytes=64)
+        bsc = const.tile([P, P], U8, name="bsc", align_bytes=64)
         nc.vector.quantize_mx(out=ac[:].bitcast(FP8X4), scales=asc[:], in_=ag[:])
         nc.vector.quantize_mx(out=bc[:].bitcast(FP8X4), scales=bsc[:], in_=bg[:])
 
@@ -137,9 +138,12 @@ def tile_dividedspacetimeattention_pa_t_kernel(tc, x, Wq, bq, k, out):
         ws = const.tile([P, E], U8, name="ws", align_bytes=64)
         nc.vector.quantize_mx(out=wc[:].bitcast(FP8X4), scales=ws[:], in_=wg[:])
 
+        def masked(b):
+            return b >= nb - 2
+
         def split(i):
             b, g0, ng = HALVES[i]
-            n = ng if i == nh - 1 else ng - 1
+            n = 1 + i % 2 if ng == 4 else 1
             return (g0, n), range(g0 + n, g0 + ng)
 
         def tp(b, w, m):
@@ -280,34 +284,56 @@ def tile_dividedspacetimeattention_pa_t_kernel(tc, x, Wq, bq, k, out):
                 op=ALU.add,
             )
 
-        def m2(i):
+        def m2(i, part):
             c, s = qc[i]
             c2, s2 = kc[i]
-            sc = ps.tile([P, 512], F32, name="sc", tag="sc", bufs=1)
-            sc_of[i] = sc
+            if part == 0:
+                sc_of[i] = ps.tile([P, 512], F32, name="sc", tag="sc", bufs=1)
+            sc = sc_of[i]
             ng = HALVES[i][2]
-            nc.tensor.matmul_mx(
-                out=sc[:, 0 : P * ng],
-                lhsT=ac[:].bitcast(FP8X4),
-                lhsT_scale=asc[:],
-                rhs=bc[:, 0 : P * ng].bitcast(FP8X4),
-                rhs_scale=bsc[:, 0 : P * ng],
-                start=True,
-                stop=False,
-            )
-            for g in range(ng):
+            late = masked(HALVES[i][0])
+            for g in range(ng // 2 * part, ng // 2 * (part + 1)):
                 nc.tensor.matmul_mx(
                     out=sc[:, P * g : P * g + P],
                     lhsT=c[:, P * g : P * g + P].bitcast(FP8X4),
                     lhsT_scale=s[:, P * g : P * g + P],
                     rhs=c2[:, P * g : P * g + P].bitcast(FP8X4),
                     rhs_scale=s2[:, P * g : P * g + P],
-                    start=False,
-                    stop=g == ng - 1,
+                    start=True,
+                    stop=not late,
                 )
+                if late:
+                    nc.tensor.matmul_mx(
+                        out=sc[:, P * g : P * g + P],
+                        lhsT=ac[:].bitcast(FP8X4),
+                        lhsT_scale=asc[:],
+                        rhs=bc[:].bitcast(FP8X4),
+                        rhs_scale=bsc[:],
+                        start=False,
+                        stop=True,
+                    )
+
+        def lift(i):
+            b, g0, ng = HALVES[i]
+            if masked(b):
+                return
+            if g0 == 0:
+                raw[b] = sb.tile([P, 8 * P], F32, name="raw", tag="raw", bufs=2)
+            nc.scalar.copy(out=raw[b][:, P * g0 : P * (g0 + ng)], in_=sc_of[i][:, 0 : P * ng])
+
+        def own(b):
+            if masked(b):
+                return
+            T = size(b)
+            s_sb[b] = sb.tile([P, 128], F32, name="s_sb", tag="s_sb", bufs=3)
+            lanes = raw[b][:, 0 : P * T].rearrange("p (l c) -> p l c", c=P)
+            for s in range(0, P, 16):
+                nc.sync.dma_start(out=vec(s_sb[b], T)[s : s + 16, :, :], in_=lanes[s : s + 16, :, s : s + 16])
 
         def red(i):
             b, g0, ng = HALVES[i]
+            if not masked(b):
+                return
             if g0 == 0:
                 s_sb[b] = sb.tile([P, 128], F32, name="s_sb", tag="s_sb", bufs=3)
             nc.vector.tensor_reduce(
@@ -373,8 +399,8 @@ def tile_dividedspacetimeattention_pa_t_kernel(tc, x, Wq, bq, k, out):
             if 0 <= i < nh:
                 f(i, *args)
 
-        def onb(f, i):
-            if 0 <= i < nh and HALVES[i][1] + HALVES[i][2] == size(HALVES[i][0]):
+        def onb(f, i, late):
+            if 0 <= i < nh and HALVES[i][1] + HALVES[i][2] == size(HALVES[i][0]) and masked(HALVES[i][0]) == late:
                 f(HALVES[i][0])
 
         def turns(i):
@@ -393,43 +419,54 @@ def tile_dividedspacetimeattention_pa_t_kernel(tc, x, Wq, bq, k, out):
             cp(0, "x", m)
         qx(0)
 
-        for i in range(nh + 8):
+        for i in range(nh + 11):
             todo = turns(i)
             first = todo[: len(todo) // 2]
             on(new_q, i)
             on(m1v, i, 0)
             on(m1s, i, 0)
-            on(m1s, i, 1)
             on(act, i, 0)
-            on(act, i, 1)
+            on(m2, i - 2, 0)
             for t in first:
                 tp(*t)
                 cp(*t)
-            onb(smax, i - 3)
             on(vd, i, 0)
-            onb(sub, i - 3)
             on(qq, i - 1)
-            on(m2, i - 2)
-            on(m1s, i, 2)
+            on(qx, i + 1)
+            on(m2, i - 2, 1)
+            on(lift, i - 2)
+            onb(own, i - 2, False)
             on(m1v, i, 1)
+            on(m1v, i, 2)
+            on(m1s, i, 1)
+            on(act, i, 1)
+            on(m1s, i, 2)
             on(m1s, i, 3)
             on(act, i, 2)
             on(act, i, 3)
             on(vd, i, 1)
-            on(qx, i + 1)
-            onb(recip, i - 6)
-            on(red, i - 2)
-            onb(finish, i - 6)
+            onb(smax, i - 5, False)
+            onb(smax, i - 3, True)
             on(qk, i - 1)
-            onb(ssum, i - 5)
+            onb(sub, i - 5, False)
+            onb(sub, i - 3, True)
+            on(vd, i, 2)
+            onb(recip, i - 8, False)
+            onb(recip, i - 6, True)
+            on(red, i - 2)
             on(rg, i)
+            onb(finish, i - 8, False)
+            onb(finish, i - 6, True)
+            onb(ssum, i - 7, False)
+            onb(ssum, i - 5, True)
             for t in todo[len(first) :]:
                 tp(*t)
                 cp(*t)
-            onb(expo, i - 4)
+            onb(expo, i - 6, False)
+            onb(expo, i - 4, True)
             if i < nh:
                 b, g0, ng = HALVES[i]
                 if g0 == 0 and b + 3 < nb:
                     load_x(b + 3, 1)
-                if g0 + ng == size(b) and b + 3 < nb:
-                    load_k(b + 3)
+                if g0 == 0 and 0 < b and b + 2 < nb:
+                    load_k(b + 2)

@@ -20,7 +20,7 @@ FLOPS = 2 * 12544 * 512 * 512 + 2 * 784 * 16 * 16 * 512
 
 BIG = 2.0 ** 100
 
-BLOCKS = [(8 * i, 8) for i in range(12)] + [(96, 2)]
+BLOCKS = [(0, 4), (4, 8), (12, 8), (20, 8), (28, 8), (36, 8), (44, 8), (52, 8), (60, 8), (68, 8), (76, 8), (84, 8), (92, 4), (96, 2)]
 
 
 def tile_dividedspacetimeattention_pa_t_kernel(tc, x, Wq, bq, k, out):
@@ -59,6 +59,9 @@ def tile_dividedspacetimeattention_pa_t_kernel(tc, x, Wq, bq, k, out):
 
         def size(b):
             return BLOCKS[b][1]
+
+        def width(b):
+            return size(b) + size(b + 1) if b == nb - 2 else size(b)
 
         def load_x(b, pieces):
             t0, T = BLOCKS[b]
@@ -143,11 +146,11 @@ def tile_dividedspacetimeattention_pa_t_kernel(tc, x, Wq, bq, k, out):
 
         def split(i):
             b, g0, ng = HALVES[i]
-            n = 1 + i % 2 if ng == 4 else 1
+            n = (1 + i % 2) if ng == 4 and i < nh - 4 else min(ng, 2)
             return (g0, n), range(g0 + n, g0 + ng)
 
         def tp(b, w, m):
-            tr = ps.tile([P, 512], F32, name="tr", tag="tr", bufs=4)
+            tr = ps.tile([P, 512], F32, name="tr", tag="tr", bufs=3)
             src = (x_sb if w == "x" else k_sb)[b][:].bitcast(F32)
             trv = tr[:].rearrange("p (u c s f) -> p u c s f", u=2, c=8, s=2, f=16)
             for s in range(2):
@@ -218,16 +221,24 @@ def tile_dividedspacetimeattention_pa_t_kernel(tc, x, Wq, bq, k, out):
                 stop=True,
             )
 
+        def plan(i, group):
+            if not 0 <= i < nh:
+                return []
+            ns, nv = split(i)[0][1], len(split(i)[1])
+            banks = [("v", v) for v in range(nv)] + [("s", u) for u in range(4 // per_bank(i) if ns else 0)]
+            if ns in (1, 2) and nv:
+                banks = [("v", 0), ("s", 0)] + [k for k in banks if k[1] > 0]
+            cut = (len(banks) + 1) // 2
+            return banks[:cut] if group == 0 else banks[cut:]
+
         def per_bank(i):
-            return {1: 4, 2: 2, 3: 1, 4: 1}[split(i)[0][1]]
+            return {0: 4, 1: 4, 2: 2, 3: 1, 4: 1}[split(i)[0][1]]
 
         def m1s(i, u):
             (g0, ng), gv = split(i)
             n = P * ng
             per = per_bank(i)
-            if per * u >= 4:
-                return
-            y = ps.tile([P, 512], F32, name="y", tag="y", bufs=3)
+            y = ps.tile([P, 512], F32, name="y", tag="y", bufs=4)
             for j in range(per * u, per * u + per):
                 o = n * (j % per)
                 lo = 0
@@ -241,8 +252,6 @@ def tile_dividedspacetimeattention_pa_t_kernel(tc, x, Wq, bq, k, out):
             (g0, ng), gv = split(i)
             n = P * ng
             per = per_bank(i)
-            if per * u >= 4:
-                return
             if u == 0:
                 qp[i] = sb.tile([P, 4, n], BF16, name="qp%d" % ng, tag="qp%d" % ng, bufs=2)
             for j in range(per * u, per * u + per):
@@ -260,22 +269,20 @@ def tile_dividedspacetimeattention_pa_t_kernel(tc, x, Wq, bq, k, out):
 
         def rg(i):
             (g0, ng), gv = split(i)
+            if ng == 0:
+                return
             nc.vector.tensor_copy(
                 out=qg[i][:, 0 : E * ng].rearrange("p (c i j) -> p c j i", i=4, j=4),
                 in_=qp[i][:].rearrange("p j (c i) -> p c j i", i=4),
             )
 
         def m1v(i, v):
-            if v >= len(split(i)[1]):
-                return
-            y = ps.tile([P, 512], F32, name="y", tag="y", bufs=3)
+            y = ps.tile([P, 512], F32, name="y", tag="y", bufs=4)
             for j in range(4):
                 m1_pass(i, y, P * j, j, split(i)[1][v], P)
             y_of[(i, 4 + v)] = y
 
         def vd(i, v):
-            if v >= len(split(i)[1]):
-                return
             o = E * (split(i)[1][v] - HALVES[i][1])
             nc.vector.tensor_tensor(
                 out=qg[i][:, o : o + E].rearrange("p (q j) -> p q j", j=4),
@@ -288,7 +295,10 @@ def tile_dividedspacetimeattention_pa_t_kernel(tc, x, Wq, bq, k, out):
             c, s = qc[i]
             c2, s2 = kc[i]
             if part == 0:
-                sc_of[i] = ps.tile([P, 512], F32, name="sc", tag="sc", bufs=1)
+                if i >= nh - 2:
+                    sc_of[i] = ps.tile([P, 512], F32, name="tr", tag="tr", bufs=3)
+                else:
+                    sc_of[i] = ps.tile([P, 512], F32, name="sc", tag="sc", bufs=1)
             sc = sc_of[i]
             ng = HALVES[i][2]
             late = masked(HALVES[i][0])
@@ -334,10 +344,11 @@ def tile_dividedspacetimeattention_pa_t_kernel(tc, x, Wq, bq, k, out):
             b, g0, ng = HALVES[i]
             if not masked(b):
                 return
-            if g0 == 0:
-                s_sb[b] = sb.tile([P, 128], F32, name="s_sb", tag="s_sb", bufs=3)
+            l0 = BLOCKS[b][0] - BLOCKS[nb - 2][0] + g0
+            if l0 == 0:
+                s_sb[nb - 2] = sb.tile([P, 128], F32, name="s_sb", tag="s_sb", bufs=3)
             nc.vector.tensor_reduce(
-                out=s_sb[b][:, 16 * g0 : 16 * (g0 + ng)].rearrange("p (l g) -> p l g", g=16),
+                out=s_sb[nb - 2][:, 16 * l0 : 16 * (l0 + ng)].rearrange("p (l g) -> p l g", g=16),
                 in_=sc_of[i][:, 0 : P * ng].rearrange("p (l t g) -> p l g t", t=8, g=16),
                 axis=AX.X,
                 op=ALU.max,
@@ -347,15 +358,15 @@ def tile_dividedspacetimeattention_pa_t_kernel(tc, x, Wq, bq, k, out):
             return t[:, 0 : 16 * n].rearrange("p (l g) -> p l g", g=16)
 
         def smax(b):
-            T = size(b)
+            T = width(b)
             mx = sb.tile([P, 8], F32, name="mx", tag="mx", bufs=2)
             nc.vector.tensor_reduce(out=mx[:, 0:T], in_=vec(s_sb[b], T), axis=AX.X, op=ALU.max)
             mx_sb[b] = mx
 
         def sub(b):
-            T = size(b)
+            T = width(b)
             d = sb.tile([P, 128], F32, name="d_sb", tag="d_sb", bufs=2)
-            nc.gpsimd.tensor_tensor(
+            (nc.vector if b >= nb - 5 else nc.gpsimd).tensor_tensor(
                 out=vec(d, T),
                 in0=vec(s_sb[b], T),
                 in1=mx_sb[b][:, 0:T].unsqueeze(2).to_broadcast([P, T, 16]),
@@ -364,109 +375,178 @@ def tile_dividedspacetimeattention_pa_t_kernel(tc, x, Wq, bq, k, out):
             d_sb[b] = d
 
         def expo(b):
-            n = 16 * size(b)
+            n = 16 * width(b)
             ex = sb.tile([P, 128], F32, name="e_sb", tag="e_sb", bufs=2)
             nc.scalar.activation(out=ex[:, 0:n], in_=d_sb[b][:, 0:n], func=ACT.Exp, scale=0.125)
             e_sb[b] = ex
 
         def ssum(b):
-            T = size(b)
+            T = width(b)
             z = sb.tile([P, 8], F32, name="z", tag="z", bufs=2)
             nc.vector.tensor_reduce(out=z[:, 0:T], in_=vec(e_sb[b], T), axis=AX.X, op=ALU.add)
             r_sb[b] = z
 
         def recip(b):
-            T = size(b)
+            T = width(b)
             r = sb.tile([P, 8], F32, name="r", tag="r", bufs=2)
             nc.vector.reciprocal(out=r[:, 0:T], in_=r_sb[b][:, 0:T])
             r_sb[b] = r
 
         def finish(b):
-            t0, T = BLOCKS[b]
-            L = 8 // T
-            o = sb.tile([P, 128], F32, name="o_sb", tag="o_sb", bufs=3)
-            nc.gpsimd.tensor_tensor(
+            T = width(b)
+            o = sb.tile([P, 128], F32, name="o_sb", tag="o_sb", bufs=6)
+            (nc.vector if b >= nb - 5 else nc.gpsimd).tensor_tensor(
                 out=vec(o, T),
                 in0=vec(e_sb[b], T),
                 in1=r_sb[b][:, 0:T].unsqueeze(2).to_broadcast([P, T, 16]),
                 op=ALU.mult,
             )
-            rows = ov[16 * t0 : 16 * (t0 + T), :, :].rearrange("r (h l) g -> l r h g", l=L)
-            for l in range(L):
-                nc.sync.dma_start(out=rows[l], in_=vec(o, T)[16 * T * l : 16 * T * (l + 1), :, :])
+            l0 = 0
+            while l0 < T:
+                t0, n = BLOCKS[b]
+                L = 8 // n
+                rows = ov[16 * t0 : 16 * (t0 + n), :, :].rearrange("r (h l) g -> l r h g", l=L)
+                for l in range(L):
+                    (nc.scalar if l % 2 and b >= nb - 2 else nc.sync).dma_start(
+                        out=rows[l],
+                        in_=vec(o, T)[16 * n * l : 16 * n * (l + 1), l0 : l0 + n, :],
+                    )
+                l0 += n
+                b += 1
 
         def on(f, i, *args):
             if 0 <= i < nh:
                 f(i, *args)
 
-        def onb(f, i, late):
-            if 0 <= i < nh and HALVES[i][1] + HALVES[i][2] == size(HALVES[i][0]) and masked(HALVES[i][0]) == late:
+        def onb(f, i):
+            if 0 <= i < nh and HALVES[i][1] + HALVES[i][2] == size(HALVES[i][0]) and not masked(HALVES[i][0]):
                 f(HALVES[i][0])
 
-        def turns(i):
-            if i >= nh:
-                return []
-            b, g0, ng = HALVES[i]
-            todo = []
-            if g0 == 0 and b + 1 < nb:
-                todo += [(b + 1, "x", m) for m in range(size(b + 1) // 2)]
-            if g0 + ng == size(b):
-                todo += [(b, "k", m) for m in range(size(b) // 2)]
-            return todo
+        def fill(i, group):
+            for kind, u in plan(i, group):
+                if kind == "v":
+                    m1v(i, u)
+                else:
+                    m1s(i, u)
+                    act(i, u)
 
-        for m in range(size(0) // 2):
-            tp(0, "x", m)
-            cp(0, "x", m)
-        qx(0)
+        def add(i, group, k):
+            lanes = [u for kind, u in plan(i, group) if kind == "v"]
+            if k < len(lanes):
+                vd(i, lanes[k])
 
-        for i in range(nh + 11):
-            todo = turns(i)
-            first = todo[: len(todo) // 2]
-            on(new_q, i)
-            on(m1v, i, 0)
-            on(m1s, i, 0)
-            on(act, i, 0)
-            on(m2, i - 2, 0)
+        steps = [(0, "x", m) for m in range(size(0) // 2)]
+        for b in range(nb):
+            if b + 1 < nb:
+                steps += [(b + 1, "x", m) for m in range(size(b + 1) // 2)]
+            steps += [(b, "k", m) for m in range(size(b) // 2)]
+        lead = size(0) // 2 + 2
+        runs = [steps[j : j + 2] for j in range(lead, len(steps), 2)]
+        for t in steps[:lead]:
+            tp(*t)
+            cp(*t)
+            if t == (0, "x", size(0) // 2 - 1):
+                qx(0)
+
+        for i in range(nh - 2):
+            first, second = (runs[2 * i : 2 * i + 2] + [[], []])[:2]
+            new_q(i)
+            fill(i, 0)
+            even = len(plan(i, 0)) < 3
+            if even:
+                on(m2, i - 2, 0)
             for t in first:
                 tp(*t)
                 cp(*t)
-            on(vd, i, 0)
-            on(qq, i - 1)
+            add(i, 0, 0)
+            on(rg, i - 1)
             on(qx, i + 1)
+            on(qq, i - 1)
+            if not even:
+                on(m2, i - 2, 0)
             on(m2, i - 2, 1)
             on(lift, i - 2)
-            onb(own, i - 2, False)
-            on(m1v, i, 1)
-            on(m1v, i, 2)
-            on(m1s, i, 1)
-            on(act, i, 1)
-            on(m1s, i, 2)
-            on(m1s, i, 3)
-            on(act, i, 2)
-            on(act, i, 3)
-            on(vd, i, 1)
-            onb(smax, i - 5, False)
-            onb(smax, i - 3, True)
+            onb(own, i - 2)
+            fill(i, 1)
+            add(i, 0, 1)
+            add(i, 1, 0)
+            onb(smax, i - 5)
             on(qk, i - 1)
-            onb(sub, i - 5, False)
-            onb(sub, i - 3, True)
-            on(vd, i, 2)
-            onb(recip, i - 8, False)
-            onb(recip, i - 6, True)
-            on(red, i - 2)
-            on(rg, i)
-            onb(finish, i - 8, False)
-            onb(finish, i - 6, True)
-            onb(ssum, i - 7, False)
-            onb(ssum, i - 5, True)
-            for t in todo[len(first) :]:
+            onb(sub, i - 5)
+            add(i, 1, 1)
+            onb(recip, i - 8)
+            onb(finish, i - 8)
+            onb(ssum, i - 7)
+            for t in second:
                 tp(*t)
                 cp(*t)
-            onb(expo, i - 6, False)
-            onb(expo, i - 4, True)
-            if i < nh:
-                b, g0, ng = HALVES[i]
-                if g0 == 0 and b + 3 < nb:
-                    load_x(b + 3, 1)
-                if g0 == 0 and 0 < b and b + 2 < nb:
-                    load_k(b + 2)
+            onb(expo, i - 6)
+            b, g0, ng = HALVES[i]
+            if g0 == 0 and b + 3 < nb:
+                load_x(b + 3, 1)
+            if g0 == 0 and 0 < b and b + 2 < nb:
+                load_k(b + 2)
+
+        pen, end, last = nh - 2, nh - 1, nb - 2
+        new_q(pen)
+        fill(pen, 0)
+        m2(pen - 2, 0)
+        for t in [t for r in runs[2 * pen :] for t in r]:
+            tp(*t)
+            cp(*t)
+        add(pen, 0, 0)
+        rg(pen - 1)
+        qx(end)
+        qq(pen - 1)
+        m2(pen - 2, 1)
+        lift(pen - 2)
+        fill(pen, 1)
+        add(pen, 1, 0)
+        qk(pen - 1)
+        smax(last - 3)
+        sub(last - 3)
+        new_q(end)
+        fill(end, 0)
+        fill(end, 1)
+        add(end, 0, 0)
+        rg(pen)
+        m2(pen - 1, 0)
+        m2(pen - 1, 1)
+        expo(last - 3)
+        lift(pen - 1)
+        own(last - 1)
+        ssum(last - 4)
+        qk(pen)
+        qk(end)
+        qq(pen)
+        m2(pen, 0)
+        m2(pen, 1)
+        recip(last - 4)
+        finish(last - 4)
+        rg(end)
+        smax(last - 2)
+        ssum(last - 3)
+        qq(end)
+        m2(end, 0)
+        m2(end, 1)
+        sub(last - 2)
+        recip(last - 3)
+        red(pen)
+        finish(last - 3)
+        expo(last - 2)
+        smax(last - 1)
+        red(end)
+        sub(last - 1)
+        ssum(last - 2)
+        smax(last)
+        recip(last - 2)
+        sub(last)
+        expo(last - 1)
+        expo(last)
+        finish(last - 2)
+        ssum(last - 1)
+        ssum(last)
+        recip(last - 1)
+        recip(last)
+        finish(last - 1)
+        finish(last)

@@ -146,7 +146,7 @@ def tile_dividedspacetimeattention_pa_t_kernel(tc, x, Wq, bq, k, out):
 
         def split(i):
             b, g0, ng = HALVES[i]
-            n = (1 + i % 2) if ng == 4 and i < nh - 4 else min(ng, 2)
+            n = (1, 1, 2)[i % 3] if i < nh - 2 else 2
             return (g0, n), range(g0 + n, g0 + ng)
 
         def tp(b, w, m):
@@ -295,7 +295,7 @@ def tile_dividedspacetimeattention_pa_t_kernel(tc, x, Wq, bq, k, out):
             c, s = qc[i]
             c2, s2 = kc[i]
             if part == 0:
-                if i >= nh - 2:
+                if i >= nh - 3:
                     sc_of[i] = ps.tile([P, 512], F32, name="tr", tag="tr", bufs=3)
                 else:
                     sc_of[i] = ps.tile([P, 512], F32, name="sc", tag="sc", bufs=1)
@@ -501,23 +501,23 @@ def tile_dividedspacetimeattention_pa_t_kernel(tc, x, Wq, bq, k, out):
         m2(pen - 2, 1)
         lift(pen - 2)
         fill(pen, 1)
-        add(pen, 1, 0)
         qk(pen - 1)
-        smax(last - 3)
-        sub(last - 3)
+        add(pen, 1, 0)
+        m2(pen - 1, 0)
+        m2(pen - 1, 1)
+        lift(pen - 1)
+        own(last - 1)
         new_q(end)
         fill(end, 0)
         fill(end, 1)
         add(end, 0, 0)
-        rg(pen)
-        m2(pen - 1, 0)
-        m2(pen - 1, 1)
-        expo(last - 3)
-        lift(pen - 1)
-        own(last - 1)
-        ssum(last - 4)
         qk(pen)
+        smax(last - 3)
         qk(end)
+        sub(last - 3)
+        rg(pen)
+        expo(last - 3)
+        ssum(last - 4)
         qq(pen)
         m2(pen, 0)
         m2(pen, 1)
@@ -532,16 +532,16 @@ def tile_dividedspacetimeattention_pa_t_kernel(tc, x, Wq, bq, k, out):
         sub(last - 2)
         recip(last - 3)
         red(pen)
-        finish(last - 3)
         expo(last - 2)
+        finish(last - 3)
         smax(last - 1)
         red(end)
         sub(last - 1)
         ssum(last - 2)
         smax(last)
+        expo(last - 1)
         recip(last - 2)
         sub(last)
-        expo(last - 1)
         expo(last)
         finish(last - 2)
         ssum(last - 1)

from contextlib import ExitStack

import concourse.mybir as mybir
from concourse.masks import make_identity

F32 = mybir.dt.float32
BF16 = mybir.dt.bfloat16
U32 = mybir.dt.uint32
U8 = mybir.dt.uint8
FP8X4 = mybir.dt.float8_e4m3fn_x4
ALU = mybir.AluOpType
ACT = mybir.ActivationFunctionType
AX = mybir.AxisListType

P = 128
E = 512
STEPS = 98
FLOPS = 2 * 12544 * 512 * 512 + 2 * 784 * 16 * 16 * 512


BIG = 2.0 ** 100

BLOCKS = [(0, 4), (4, 8), (12, 8), (20, 8), (28, 8), (36, 8), (44, 8), (52, 8), (60, 8), (68, 8), (76, 8), (84, 8), (92, 4), (96, 2)]


def tile_dividedspacetimeattention_pa_t_kernel(tc, x, Wq, bq, k, out):
    nc = tc.nc
    nb = len(BLOCKS)
    HALVES = [(b, g, min(4, T)) for b, (t0, T) in enumerate(BLOCKS) for g in range(0, T, 4)]
    nh = len(HALVES)
    xv = x.rearrange("b (q t) e -> (b q) t e", t=STEPS)
    kv = k.rearrange("b h (j t) g e -> (t g) (b h j) e", j=2, t=STEPS)
    ov = out.rearrange("b h (j t) f g -> (t f) (b h j) g", j=2, t=STEPS)

    with ExitStack() as ctx:
        const = ctx.enter_context(tc.tile_pool(name="const", bufs=1))
        sb = ctx.enter_context(tc.tile_pool(name="sb", bufs=2))
        ps = ctx.enter_context(tc.psum_pool(name="ps", bufs=1))
        ctx.enter_context(tc.manual_schedule())

        x_sb = {}
        k_sb = {}
        xg = {}
        kg = {}
        xc = {}
        kc = {}
        qp = {}
        qg = {}
        qc = {}
        raw = {}
        s_sb = {}
        d_sb = {}
        e_sb = {}
        mx_sb = {}
        r_sb = {}
        tr_of = {}
        y_of = {}
        sc_of = {}

        def size(b):
            return BLOCKS[b][1]

        def width(b):
            return size(b) + size(b + 1) if b == nb - 2 else size(b)

        def load_x(b, pieces):
            t0, T = BLOCKS[b]
            xt = sb.tile([P, 8 * E], BF16, name="x_sb", tag="x_sb", bufs=3)
            n = T // pieces
            for a in range(0, T, n):
                nc.sync.dma_start(
                    out=xt[:, E * a : E * (a + n)].rearrange("p (t e) -> p t e", e=E),
                    in_=xv[:, t0 + a : t0 + a + n, :],
                )
            x_sb[b] = xt

        def load_k(b):
            t0, T = BLOCKS[b]
            L = 8 // T
            kt = sb.tile([P, 8 * E], BF16, name="k_sb", tag="k_sb", bufs=3)
            k3 = kt[:, 0 : E * T].rearrange("p (h e) -> p h e", e=E)
            rows = kv[16 * t0 : 16 * (t0 + T), :, :].rearrange("r (h l) e -> l r h e", l=L)
            for l in range(L):
                nc.sync.dma_start(out=k3[16 * T * l : 16 * T * (l + 1), :, :], in_=rows[l])
            k_sb[b] = kt

        wraw = const.tile([P, 4, E], BF16, name="wraw")
        nc.sync.dma_start(out=wraw[:], in_=Wq.rearrange("(p j) n -> p j n", j=4))
        b_bf = const.tile([P, 4], BF16, name="b_bf")
        nc.scalar.dma_start(out=b_bf[:], in_=bq.rearrange("(p j) -> p j", j=4))
        load_x(0, size(0) // 2)
        load_x(1, 2)
        load_k(0)
        load_x(2, 1)
        load_k(1)
        load_k(2)

        ident = const.tile([P, P], F32, name="ident")
        make_identity(nc, ident[:])
        zero = const.tile([P, 8], F32, name="zero")
        nc.vector.memset(zero[:], 0.0)
        warm = const.tile([P, 8], F32, name="warm")
        nc.scalar.activation(out=warm[:], in_=zero[:], func=ACT.Exp)

        perm = const.tile([P, P], F32, name="perm")
        nc.vector.tensor_copy(
            out=perm[:].rearrange("p (b j f) -> p b j f", b=4, j=2, f=16),
            in_=ident[:].rearrange("p (b f j) -> p b j f", b=4, f=16, j=2),
        )
        ag = const.tile([P, 4 * P], BF16, name="ag", align_bytes=64)
        bg = const.tile([P, 4 * P], BF16, name="bg", align_bytes=64)
        nc.gpsimd.memset(ag[:], 0.0)
        nc.gpsimd.memset(bg[:], 0.0)
        slot = ident[:, 0:8].unsqueeze(2).to_broadcast([P, 8, 16])
        nc.vector.tensor_copy(
            out=ag[:].rearrange("p (s f j) -> p s f j", s=8, f=16, j=4)[:, :, :, 0], in_=slot
        )
        nc.vector.tensor_scalar(
            out=bg[:].rearrange("p (s f j) -> p s f j", s=8, f=16, j=4)[:, :, :, 0],
            in0=slot,
            scalar1=-1.0,
            scalar2=BIG,
            op0=ALU.add,
            op1=ALU.mult,
        )
        ac = const.tile([P, P], U32, name="ac", align_bytes=64)
        asc = const.tile([P, P], U8, name="asc", align_bytes=64)
        bc = const.tile([P, P], U32, name="bc", align_bytes=64)
        bsc = const.tile([P, P], U8, name="bsc", align_bytes=64)
        nc.vector.quantize_mx(out=ac[:].bitcast(FP8X4), scales=asc[:], in_=ag[:])
        nc.vector.quantize_mx(out=bc[:].bitcast(FP8X4), scales=bsc[:], in_=bg[:])

        b32 = const.tile([P, 4], F32, name="b32")
        nc.vector.tensor_copy(out=b32[:], in_=b_bf[:])
        wg = const.tile([P, 4 * E], BF16, name="wg", align_bytes=64)
        wgv = wg[:].rearrange("p (t m j) -> p t m j", t=4, m=P, j=4)
        wrv = wraw[:].rearrange("p j (m t) -> p t m j", m=P, t=4)
        for t in range(4):
            nc.vector.tensor_copy(out=wgv[:, t], in_=wrv[:, t])
        wc = const.tile([P, E], U32, name="wc", align_bytes=64)
        ws = const.tile([P, E], U8, name="ws", align_bytes=64)
        nc.vector.quantize_mx(out=wc[:].bitcast(FP8X4), scales=ws[:], in_=wg[:])

        def masked(b):
            return b >= nb - 2

        def split(i):
            b, g0, ng = HALVES[i]
            n = (1, 1, 2)[i % 3] if i < nh - 2 else 2
            return (g0, n), range(g0 + n, g0 + ng)

        def tp(b, w, m):
            tr = ps.tile([P, 512], F32, name="tr", tag="tr", bufs=3)
            src = (x_sb if w == "x" else k_sb)[b][:].bitcast(F32)
            trv = tr[:].rearrange("p (u c s f) -> p u c s f", u=2, c=8, s=2, f=16)
            for s in range(2):
                for u in range(2):
                    c0 = 256 * (2 * m + s)
                    words = src[:, c0 + u : c0 + 256 : 2]
                    if w == "x":
                        nc.tensor.transpose(trv[:, u, :, s, :], words, perm[:])
                    else:
                        o = 256 * s + 128 * u
                        nc.tensor.transpose(tr[:, o : o + 128], words, ident[:])
            tr_of[(w, b, m)] = tr

        def cp(b, w, m):
            T = size(b)
            if w == "x":
                if m == 0:
                    xg[b] = sb.tile([P, 8 * E], BF16, name="xg", tag="xg", bufs=3, align_bytes=64)
                gv = xg[b][:].bitcast(F32)[:, 0 : 256 * T].rearrange(
                    "p (c m q u) -> p c m q u", c=8, m=T // 2, q=32, u=2
                )
                nc.scalar.copy(
                    out=gv[:, :, m, :, :],
                    in_=tr_of[(w, b, m)][:].rearrange("p (u c q) -> p c q u", u=2, c=8, q=32),
                )
            else:
                if m == 0:
                    kg[b] = sb.tile([P, 8 * E], BF16, name="kg", tag="kg", bufs=3, align_bytes=64)
                nc.scalar.copy(
                    out=kg[b][:].bitcast(F32)[:, 512 * m : 512 * m + 512].rearrange(
                        "p (s q u) -> p s q u", s=2, q=P, u=2
                    ),
                    in_=tr_of[(w, b, m)][:].rearrange("p (s u q) -> p s q u", s=2, u=2, q=P),
                )

        def quant(src, i, store, tag, bufs):
            b, g0, ng = HALVES[i]
            c = sb.tile([P, 512], U32, name=tag + "c", tag=tag + "c", bufs=bufs, align_bytes=64)
            s = sb.tile([P, 512], U8, name=tag + "s", tag=tag + "s", bufs=bufs, align_bytes=64)
            nc.vector.quantize_mx(
                out=c[:, 0 : P * ng].bitcast(FP8X4),
                scales=s[:, 0 : P * ng],
                in_=src[:, 0 : E * ng],
            )
            store[i] = (c, s)

        def qx(i):
            b, g0, ng = HALVES[i]
            quant(xg[b][:, E * g0 : E * (g0 + ng)], i, xc, "x", 2)

        def qk(i):
            b, g0, ng = HALVES[i]
            quant(kg[b][:, E * g0 : E * (g0 + ng)], i, kc, "k", 4)

        def qq(i):
            quant(qg[i], i, qc, "q", 3)

        def m1_pass(i, y, o, j, g, n):
            c, s = xc[i]
            o0 = P * (g - HALVES[i][1])
            nc.tensor.matmul_mx(
                out=y[:, o : o + n],
                lhsT=wc[:, P * j : P * j + P].bitcast(FP8X4),
                lhsT_scale=ws[:, P * j : P * j + P],
                rhs=c[:, o0 : o0 + n].bitcast(FP8X4),
                rhs_scale=s[:, o0 : o0 + n],
                start=True,
                stop=True,
            )

        def plan(i, group):
            if not 0 <= i < nh:
                return []
            ns, nv = split(i)[0][1], len(split(i)[1])
            banks = [("v", v) for v in range(nv)] + [("s", u) for u in range(4 // per_bank(i) if ns else 0)]
            if ns in (1, 2) and nv:
                banks = [("v", 0), ("s", 0)] + [k for k in banks if k[1] > 0]
            cut = (len(banks) + 1) // 2
            return banks[:cut] if group == 0 else banks[cut:]

        def per_bank(i):
            return {0: 4, 1: 4, 2: 2, 3: 1, 4: 1}[split(i)[0][1]]

        def m1s(i, u):
            (g0, ng), gv = split(i)
            n = P * ng
            per = per_bank(i)
            y = ps.tile([P, 512], F32, name="y", tag="y", bufs=4)
            for j in range(per * u, per * u + per):
                o = n * (j % per)
                lo = 0
                for ln in (4, 2, 1):
                    if lo + ln <= ng:
                        m1_pass(i, y, o + P * lo, j, g0 + lo, P * ln)
                        lo += ln
            y_of[(i, u)] = y

        def act(i, u):
            (g0, ng), gv = split(i)
            n = P * ng
            per = per_bank(i)
            if u == 0:
                qp[i] = sb.tile([P, 4, n], BF16, name="qp%d" % ng, tag="qp%d" % ng, bufs=2)
            for j in range(per * u, per * u + per):
                o = n * (j % per)
                nc.scalar.activation(
                    out=qp[i][:, j, :],
                    in_=y_of[(i, u)][:, o : o + n],
                    func=ACT.Identity,
                    bias=b32[:, j : j + 1],
                    scale=1.0,
                )

        def new_q(i):
            qg[i] = sb.tile([P, 4 * E], BF16, name="qg", tag="qg", bufs=3, align_bytes=64)

        def rg(i):
            (g0, ng), gv = split(i)
            if ng == 0:
                return
            nc.vector.tensor_copy(
                out=qg[i][:, 0 : E * ng].rearrange("p (c i j) -> p c j i", i=4, j=4),
                in_=qp[i][:].rearrange("p j (c i) -> p c j i", i=4),
            )

        def m1v(i, v):
            y = ps.tile([P, 512], F32, name="y", tag="y", bufs=4)
            for j in range(4):
                m1_pass(i, y, P * j, j, split(i)[1][v], P)
            y_of[(i, 4 + v)] = y

        def vd(i, v):
            o = E * (split(i)[1][v] - HALVES[i][1])
            nc.vector.tensor_tensor(
                out=qg[i][:, o : o + E].rearrange("p (q j) -> p q j", j=4),
                in0=y_of[(i, 4 + v)][:].rearrange("p (j q) -> p q j", j=4),
                in1=b32[:].unsqueeze(1).to_broadcast([P, P, 4]),
                op=ALU.add,
            )

        def m2(i, part):
            c, s = qc[i]
            c2, s2 = kc[i]
            if part == 0:
                if i >= nh - 3:
                    sc_of[i] = ps.tile([P, 512], F32, name="tr", tag="tr", bufs=3)
                else:
                    sc_of[i] = ps.tile([P, 512], F32, name="sc", tag="sc", bufs=1)
            sc = sc_of[i]
            ng = HALVES[i][2]
            late = masked(HALVES[i][0])
            for g in range(ng // 2 * part, ng // 2 * (part + 1)):
                nc.tensor.matmul_mx(
                    out=sc[:, P * g : P * g + P],
                    lhsT=c[:, P * g : P * g + P].bitcast(FP8X4),
                    lhsT_scale=s[:, P * g : P * g + P],
                    rhs=c2[:, P * g : P * g + P].bitcast(FP8X4),
                    rhs_scale=s2[:, P * g : P * g + P],
                    start=True,
                    stop=not late,
                )
                if late:
                    nc.tensor.matmul_mx(
                        out=sc[:, P * g : P * g + P],
                        lhsT=ac[:].bitcast(FP8X4),
                        lhsT_scale=asc[:],
                        rhs=bc[:].bitcast(FP8X4),
                        rhs_scale=bsc[:],
                        start=False,
                        stop=True,
                    )

        def lift(i):
            b, g0, ng = HALVES[i]
            if masked(b):
                return
            if g0 == 0:
                raw[b] = sb.tile([P, 8 * P], F32, name="raw", tag="raw", bufs=2)
            nc.scalar.copy(out=raw[b][:, P * g0 : P * (g0 + ng)], in_=sc_of[i][:, 0 : P * ng])

        def own(b):
            if masked(b):
                return
            T = size(b)
            s_sb[b] = sb.tile([P, 128], F32, name="s_sb", tag="s_sb", bufs=3)
            lanes = raw[b][:, 0 : P * T].rearrange("p (l c) -> p l c", c=P)
            for s in range(0, P, 16):
                nc.sync.dma_start(out=vec(s_sb[b], T)[s : s + 16, :, :], in_=lanes[s : s + 16, :, s : s + 16])

        def red(i):
            b, g0, ng = HALVES[i]
            if not masked(b):
                return
            l0 = BLOCKS[b][0] - BLOCKS[nb - 2][0] + g0
            if l0 == 0:
                s_sb[nb - 2] = sb.tile([P, 128], F32, name="s_sb", tag="s_sb", bufs=3)
            nc.vector.tensor_reduce(
                out=s_sb[nb - 2][:, 16 * l0 : 16 * (l0 + ng)].rearrange("p (l g) -> p l g", g=16),
                in_=sc_of[i][:, 0 : P * ng].rearrange("p (l t g) -> p l g t", t=8, g=16),
                axis=AX.X,
                op=ALU.max,
            )

        def vec(t, n):
            return t[:, 0 : 16 * n].rearrange("p (l g) -> p l g", g=16)

        def smax(b):
            T = width(b)
            mx = sb.tile([P, 8], F32, name="mx", tag="mx", bufs=2)
            nc.vector.tensor_reduce(out=mx[:, 0:T], in_=vec(s_sb[b], T), axis=AX.X, op=ALU.max)
            mx_sb[b] = mx

        def sub(b):
            T = width(b)
            d = sb.tile([P, 128], F32, name="d_sb", tag="d_sb", bufs=2)
            (nc.vector if b >= nb - 5 else nc.gpsimd).tensor_tensor(
                out=vec(d, T),
                in0=vec(s_sb[b], T),
                in1=mx_sb[b][:, 0:T].unsqueeze(2).to_broadcast([P, T, 16]),
                op=ALU.subtract,
            )
            d_sb[b] = d

        def expo(b):
            n = 16 * width(b)
            ex = sb.tile([P, 128], F32, name="e_sb", tag="e_sb", bufs=2)
            nc.scalar.activation(out=ex[:, 0:n], in_=d_sb[b][:, 0:n], func=ACT.Exp, scale=0.125)
            e_sb[b] = ex

        def ssum(b):
            T = width(b)
            z = sb.tile([P, 8], F32, name="z", tag="z", bufs=2)
            nc.vector.tensor_reduce(out=z[:, 0:T], in_=vec(e_sb[b], T), axis=AX.X, op=ALU.add)
            r_sb[b] = z

        def recip(b):
            T = width(b)
            r = sb.tile([P, 8], F32, name="r", tag="r", bufs=2)
            nc.vector.reciprocal(out=r[:, 0:T], in_=r_sb[b][:, 0:T])
            r_sb[b] = r

        def finish(b):
            T = width(b)
            o = sb.tile([P, 128], F32, name="o_sb", tag="o_sb", bufs=6)
            (nc.vector if b >= nb - 5 else nc.gpsimd).tensor_tensor(
                out=vec(o, T),
                in0=vec(e_sb[b], T),
                in1=r_sb[b][:, 0:T].unsqueeze(2).to_broadcast([P, T, 16]),
                op=ALU.mult,
            )
            l0 = 0
            while l0 < T:
                t0, n = BLOCKS[b]
                L = 8 // n
                rows = ov[16 * t0 : 16 * (t0 + n), :, :].rearrange("r (h l) g -> l r h g", l=L)
                for l in range(L):
                    (nc.scalar if l % 2 and b >= nb - 2 else nc.sync).dma_start(
                        out=rows[l],
                        in_=vec(o, T)[16 * n * l : 16 * n * (l + 1), l0 : l0 + n, :],
                    )
                l0 += n
                b += 1

        def on(f, i, *args):
            if 0 <= i < nh:
                f(i, *args)

        def onb(f, i):
            if 0 <= i < nh and HALVES[i][1] + HALVES[i][2] == size(HALVES[i][0]) and not masked(HALVES[i][0]):
                f(HALVES[i][0])

        def fill(i, group):
            for kind, u in plan(i, group):
                if kind == "v":
                    m1v(i, u)
                else:
                    m1s(i, u)
                    act(i, u)

        def add(i, group, k):
            lanes = [u for kind, u in plan(i, group) if kind == "v"]
            if k < len(lanes):
                vd(i, lanes[k])

        steps = [(0, "x", m) for m in range(size(0) // 2)]
        for b in range(nb):
            if b + 1 < nb:
                steps += [(b + 1, "x", m) for m in range(size(b + 1) // 2)]
            steps += [(b, "k", m) for m in range(size(b) // 2)]
        lead = size(0) // 2 + 2
        runs = [steps[j : j + 2] for j in range(lead, len(steps), 2)]
        for t in steps[:lead]:
            tp(*t)
            cp(*t)
            if t == (0, "x", size(0) // 2 - 1):
                qx(0)

        for i in range(nh - 2):
            first, second = (runs[2 * i : 2 * i + 2] + [[], []])[:2]
            new_q(i)
            fill(i, 0)
            even = len(plan(i, 0)) < 3
            if even:
                on(m2, i - 2, 0)
            for t in first:
                tp(*t)
                cp(*t)
            add(i, 0, 0)
            on(rg, i - 1)
            on(qx, i + 1)
            on(qq, i - 1)
            if not even:
                on(m2, i - 2, 0)
            on(m2, i - 2, 1)
            on(lift, i - 2)
            onb(own, i - 2)
            fill(i, 1)
            add(i, 0, 1)
            add(i, 1, 0)
            onb(smax, i - 5)
            on(qk, i - 1)
            onb(sub, i - 5)
            add(i, 1, 1)
            onb(recip, i - 8)
            onb(finish, i - 8)
            onb(ssum, i - 7)
            for t in second:
                tp(*t)
                cp(*t)
            onb(expo, i - 6)
            b, g0, ng = HALVES[i]
            if g0 == 0 and b + 3 < nb:
                load_x(b + 3, 1)
            if g0 == 0 and 0 < b and b + 2 < nb:
                load_k(b + 2)

        pen, end, last = nh - 2, nh - 1, nb - 2
        new_q(pen)
        fill(pen, 0)
        m2(pen - 2, 0)
        for t in [t for r in runs[2 * pen :] for t in r]:
            tp(*t)
            cp(*t)
        add(pen, 0, 0)
        rg(pen - 1)
        qx(end)
        qq(pen - 1)
        m2(pen - 2, 1)
        lift(pen - 2)
        fill(pen, 1)
        qk(pen - 1)
        add(pen, 1, 0)
        m2(pen - 1, 0)
        m2(pen - 1, 1)
        lift(pen - 1)
        own(last - 1)
        new_q(end)
        fill(end, 0)
        fill(end, 1)
        add(end, 0, 0)
        qk(pen)
        smax(last - 3)
        qk(end)
        sub(last - 3)
        rg(pen)
        expo(last - 3)
        ssum(last - 4)
        qq(pen)
        m2(pen, 0)
        m2(pen, 1)
        recip(last - 4)
        finish(last - 4)
        rg(end)
        smax(last - 2)
        ssum(last - 3)
        qq(end)
        m2(end, 0)
        m2(end, 1)
        sub(last - 2)
        recip(last - 3)
        red(pen)
        expo(last - 2)
        finish(last - 3)
        smax(last - 1)
        red(end)
        sub(last - 1)
        ssum(last - 2)
        smax(last)
        expo(last - 1)
        recip(last - 2)
        sub(last)
        expo(last)
        finish(last - 2)
        ssum(last - 1)
        ssum(last)
        recip(last - 1)
        recip(last)
        finish(last - 1)
        finish(last)
